import numpy as np
import ml_dtypes


def mxq(x, axis, fmt="e4m3"):
    dtype, down = {"e4m3": (ml_dtypes.float8_e4m3fn, 7), "e5m2": (ml_dtypes.float8_e5m2, 14)}[fmt]
    v = np.moveaxis(np.asarray(x, np.float32).astype(ml_dtypes.bfloat16).astype(np.float64), axis, -1)
    blocks = v.reshape(v.shape[:-1] + (-1, 32))
    amax = np.abs(blocks).max(-1, keepdims=True)
    byte = np.maximum(np.where(amax > 0, np.frexp(amax)[1] - 1 + 127, 0) - down, 1)
    scale = np.exp2(byte - 127.0)
    codes = (blocks / scale).astype(np.float32).astype(dtype).astype(np.float64)
    return np.moveaxis((codes * scale).reshape(v.shape), -1, axis)


WIDE = False


def mx_kscale(k):
    if not WIDE:
        return np.ones(k)
    levels = np.array([18, -18])
    if k % 512:
        return np.exp2(np.random.permutation(np.resize(levels, k // 32))).repeat(32)
    a = np.empty((k // 512, 16))
    for p in range(k // 512):
        a[p, :8] = np.random.permutation(np.resize(levels, 8))
        for g in range(8):
            far = levels[np.abs(levels - a[p, g]) >= 10]
            a[p, g + 8] = far[np.random.randint(len(far))]
    return np.exp2(a.ravel()).repeat(32)


BF16 = ml_dtypes.bfloat16


def bf(x):
    return np.asarray(x, np.float32).astype(BF16)


def f64(x):
    return np.asarray(x).astype(np.float64)


B, C, IC, H, W = 2, 1024, 512, 32, 32
N = H * W


def logits_and_lse(theta, phi, pos_embedding):
    qk = f64(theta).transpose(0, 2, 1) @ f64(phi)
    s = qk + f64(pos_embedding)
    m = s.max(1)
    lse = m + np.log(np.exp(s - m[:, None, :]).sum(1))
    return qk, lse


def setup_inputs():
    s = mx_kscale(N)
    u = mx_kscale(C)
    v = mx_kscale(IC)
    a = 1.2 * IC ** -0.25
    theta = bf(np.random.standard_normal((B, IC, N)) * a)
    phi = bf(np.random.standard_normal((B, IC, N)) * a)
    g0 = bf(np.random.standard_normal((B, IC, N)))
    pos0 = bf(np.random.standard_normal((1, N, N)))
    dec0 = bf(1.5 + 0.5 * np.random.standard_normal((1, IC, H, W)))
    w0 = bf(np.random.standard_normal((C, IC)) * 2.0 / np.sqrt(IC))
    x = bf(np.random.standard_normal((B, C, H, W)))
    go = np.random.standard_normal((B, C, N)) * np.exp2(np.random.randint(-6, 1, (B, 1, N))) * 4.0
    go = bf(go * u[None, :, None] / s[None, None, :])
    qk, lse = logits_and_lse(theta, phi, pos0)
    return {"theta": theta,
            "phi": phi,
            "g_proj": bf(f64(g0) / v[None, :, None]),
            "pos_embedding": bf(f64(pos0) + np.log(s)[None, :, None]),
            "pos_embedding_decoder": bf(f64(dec0) / v[None, :, None, None]),
            "w_mask": bf(f64(w0) * v[None, :] / u[:, None]),
            "x": x,
            "qk": np.asarray(qk, np.float32),
            "lse": np.asarray(lse, np.float32),
            "grad_out": go.reshape(B, C, H, W)}


def reference(theta, phi, g_proj, pos_embedding, pos_embedding_decoder, w_mask, x, qk, lse, grad_out):
    go = f64(grad_out).reshape(B, C, N)
    dy = mxq(go, 1, "e5m2").transpose(0, 2, 1) @ mxq(f64(w_mask), 0, "e4m3")
    attn = np.exp(f64(qk) + f64(pos_embedding) - f64(lse)[:, None, :])
    g = f64(g_proj) + f64(pos_embedding_decoder).reshape(1, IC, N)
    dattn = mxq(dy, 2, "e5m2") @ mxq(g, 1, "e4m3")
    dg = mxq(dy, 1, "e5m2").transpose(0, 2, 1) @ mxq(attn, 1, "e4m3")
    ds = attn * (dattn - (attn * dattn).sum(1, keepdims=True))
    return ds.sum(0, keepdims=True), dg

@@ -1,0 +1,397 @@
+from contextlib import ExitStack
+
+import concourse.mybir as mybir
+from concourse.masks import make_identity
+
+B, C, IC, N = 2, 1024, 512, 1024
+FLOPS = 3 * 2 * B * N * N * IC
+BYTES = 2 * (B * IC * N + N * N + IC * N + C * IC + B * C * N) + 4 * (B * N * N + B * N + N * N + B * IC * N)
+
+F32 = mybir.dt.float32
+BF16 = mybir.dt.bfloat16
+U32 = mybir.dt.uint32
+U8 = mybir.dt.uint8
+E4M3 = mybir.dt.float8_e4m3fn_x4
+E5M2 = mybir.dt.float8_e5m2_x4
+ALU = mybir.AluOpType
+ACT = mybir.ActivationFunctionType
+
+P = 128
+K = 512
+ATTN_BUFS = 16
+QK_BUFS = 4
+DA_BANKS = 4
+E1 = "V"
+E2 = "V"
+PRE = 8
+LATE = {0: 2, 1: 2, 2: 1, 3: 1, 4: 1, 5: 1}
+OUT0_RUNS = [(0, 2), (0, 2), (2, 2), (2, 2), (4, 2), (4, 2), (6, 1), (7, 1)]
+DGS = {6: 1, 7: 1, 8: 1, 9: 1, 10: 1, 11: 3, 12: 2, 13: 2, 14: 2, 15: 2}
+AQ = {5: (0, 0), 6: (1, 0), 11: (0, 1), 12: (1, 1)}
+TURN = {0: 1, 1: 2, 2: 2, 3: 2, 4: 1, 7: 2, 8: 2, 9: 2, 10: 2}
+MOV_BUFS = 3
+RAW_BUFS = 5
+
+
+def tile_nonlocalblock_pa_v_kernel(
+    tc, theta, phi, g_proj, pos_embedding, pos_embedding_decoder, w_mask, x, qk, lse, grad_out, out_0, out_1
+):
+    nc = tc.nc
+    go_hbm = grad_out.rearrange("b o h w -> b o (h w)")
+    dec_hbm = pos_embedding_decoder.rearrange("b c h w -> b c (h w)")
+
+    with ExitStack() as ctx:
+        sb = ctx.enter_context(tc.tile_pool(name="sb", bufs=1))
+        ps = ctx.enter_context(tc.psum_pool(name="ps", bufs=1))
+        ctx.enter_context(tc.manual_schedule())
+        T = {}
+
+        def rows4(tile):
+            return tile.rearrange("p (t n) -> p t n", t=4)
+
+        def load(key, src, dtype, tag, bufs):
+            width = src.shape[1]
+            T[key] = sb.tile([P, 4 * width], dtype, name=tag, tag=tag, bufs=bufs, align_bytes=64)
+            nc.sync.dma_start(out=rows4(T[key][:]), in_=src.rearrange("(p t) n -> p t n", t=4))
+
+        def load_w(q):
+            load(("w", q), w_mask[q * K:(q + 1) * K, :], BF16, "raw", RAW_BUFS)
+
+        def load_go(b, q, g):
+            load(("go", b, q, g), go_hbm[b, q * K:(q + 1) * K, g * K:(g + 1) * K], BF16, "raw", RAW_BUFS)
+
+        def load_dec():
+            load("dec", dec_hbm[0], BF16, "wide", 3)
+
+        def load_g(b):
+            load(("g", b), g_proj[b], BF16, "wide", 3)
+
+        def load_pos(g, h):
+            load(("pos", g, h), pos_embedding[0, g * K:(g + 1) * K, h * K:(h + 1) * K], BF16, "pos", 3)
+
+        def load_qk(b, g, h):
+            load(("qk", b, g, h), qk[b, g * K:(g + 1) * K, h * K:(h + 1) * K], F32, "qk", QK_BUFS)
+
+        def copy(engine, out, in_):
+            if engine == "V":
+                nc.vector.tensor_copy(out=out, in_=in_)
+            else:
+                nc.scalar.copy(out=out, in_=in_)
+
+        def staging(key):
+            T[key] = sb.tile([P, 4 * K], BF16, name="staging", tag="staging", bufs=3, align_bytes=64)
+            return T[key]
+
+        def mx_tiles(key, width, tag, bufs):
+            codes = sb.tile([P, width], U32, name=tag + "_codes", tag=tag + "_codes", bufs=bufs, align_bytes=64)
+            scales = sb.tile([P, width], U8, name=tag + "_scales", tag=tag + "_scales", bufs=bufs, align_bytes=64)
+            T[key] = (codes, scales)
+
+        def quantize(key, src, fmt, cols=slice(0, K)):
+            codes, scales = T[key]
+            nc.vector.quantize_mx(out=codes[:, cols].bitcast(fmt), scales=scales[:, cols], in_=src)
+
+        def mx(out, lhs_key, lhs_fmt, lhs_cols, rhs_key, rhs_fmt, rhs_cols, start, stop):
+            lc, lsc = T[lhs_key]
+            rc, rsc = T[rhs_key]
+            nc.tensor.matmul_mx(out=out, lhsT=lc[:, lhs_cols].bitcast(lhs_fmt), lhsT_scale=lsc[:, lhs_cols],
+                                rhs=rc[:, rhs_cols].bitcast(rhs_fmt), rhs_scale=rsc[:, rhs_cols], start=start, stop=stop)
+
+        def sc_bank(key):
+            T[key] = ps.tile([P, K], F32, name="sc", tag="sc", bufs=8 - DA_BANKS)
+            return T[key]
+
+        def interleave(engine, key, src):
+            dst = staging(key)
+            copy(engine, dst[:].rearrange("p (c i t) -> p c t i", i=4, t=4), src.rearrange("p t (c i) -> p c t i", i=4))
+
+        def w_il(q, engine):
+            dst = staging(("wi", q))
+            copy(engine, dst[:].rearrange("p (a m t) -> p m t a", a=4, t=4),
+                 T["w", q][:].rearrange("p (t m a) -> p m t a", t=4, a=4))
+
+        def w_q(q):
+            mx_tiles(("wq", q), K, "wq", 2)
+            quantize(("wq", q), T["wi", q][:], E4M3)
+
+        def go_il(b, q, g, engine):
+            interleave(engine, ("goi", b, q, g), rows4(T["go", b, q, g][:]))
+
+        def go_q(b, q, g):
+            if q == 0:
+                mx_tiles(("goq", b, g), 2 * K, "mov", MOV_BUFS)
+            quantize(("goq", b, g), T["goi", b, q, g][:], E5M2, slice(q * K, (q + 1) * K))
+
+        def dy_mm(b, g, a):
+            bank = sc_bank(("dyp", b, g, a))
+            for q in range(2):
+                mx(bank[:], ("wq", q), E4M3, slice(a * P, (a + 1) * P), ("goq", b, g), E5M2, slice(q * K, (q + 1) * K), q == 0, q == 1)
+
+        def dy_ev(b, g, a):
+            if a == 0:
+                T["dyt", b, g] = sb.tile([P, 4 * K], BF16, name="dyt", tag="dyt", bufs=2, align_bytes=64)
+            nc.scalar.copy(out=T["dyt", b, g][:, a * K:(a + 1) * K].rearrange("p (u w e) -> p u w e", u=2, e=2),
+                           in_=T["dyp", b, g, a][:].rearrange("p (w u e) -> p u w e", u=2, e=2))
+
+        def dyb_il(b, g, engine):
+            dst = staging(("dybi", b, g))
+            copy(engine, dst[:].rearrange("p (e v a) -> p v a e", e=2, a=4),
+                 T["dyt", b, g][:].rearrange("p (a v e) -> p v a e", a=4, e=2))
+
+        def dyb_q(b, g):
+            mx_tiles(("dyb", b, g), K, "dyb", 4)
+            quantize(("dyb", b, g), T["dybi", b, g][:], E5M2)
+
+        def dya_tr(b, g, pair):
+            bank = sc_bank(("dyw", b, g, pair))
+            words = T["dyt", b, g][:].bitcast(F32)
+            for s in range(4):
+                src = (4 * pair + s) * P
+                nc.tensor.transpose(bank[:, s * P:(s + 1) * P], words[:, src:src + P], ident32[:])
+
+        def dya_ev(b, g, pair):
+            if pair == 0:
+                T["dyai", b, g] = sb.tile([P, 4 * K], BF16, name="dyai", tag="dyai", bufs=2, align_bytes=64)
+            words = T["dyai", b, g][:].bitcast(F32)
+            nc.scalar.copy(out=words[:, pair * K:(pair + 1) * K].rearrange("p (a m u) -> p a m u", a=2, u=2),
+                           in_=T["dyw", b, g, pair][:].rearrange("p (a u m) -> p a m u", a=2, u=2))
+
+        def dya_q(b, g):
+            mx_tiles(("dya", b, g), K, "dya", 4)
+            quantize(("dya", b, g), T["dyai", b, g][:], E5M2)
+
+        def g_add(b):
+            nc.vector.tensor_tensor(out=T["g", b][:], in0=T["g", b][:], in1=T["dec"][:], op=ALU.add)
+
+        def g_il(b, h, engine):
+            interleave(engine, ("gi", b, h), rows4(T["g", b][:])[:, :, h * K:(h + 1) * K])
+
+        def g_q(b, h):
+            mx_tiles(("gq", b, h), K, "gq", 4)
+            quantize(("gq", b, h), T["gi", b, h][:], E4M3)
+
+        def logits(b, jt, g):
+            bank = sc_bank(("lg", b, jt, g))
+            h, j0 = jt // 4, (jt % 4) * P
+            for n in range(4):
+                t = 2 * (n % 2) + n // 2
+                nc.tensor.matmul(bank[:, n * P:(n + 1) * P], lhsT=T["pos", g, h][:, t * K + j0:t * K + j0 + P],
+                                 rhs=ident16[:], start=(n == 0), stop=False)
+            for n in range(4):
+                t = 2 * (n % 2) + n // 2
+                nc.tensor.matmul(bank[:, n * P:(n + 1) * P], lhsT=T["qk", b, g, h][:, t * K + j0:t * K + j0 + P],
+                                 rhs=ident32[:], start=False, stop=(n == 3), is_transpose=True)
+
+        def exp(b, jt, g):
+            if g == 0:
+                T["attn", b, jt] = sb.tile([P, 2 * K], F32, name="attn", tag="attn", bufs=ATTN_BUFS, align_bytes=64)
+            nc.scalar.activation(out=T["attn", b, jt][:, g * K:(g + 1) * K], in_=T["lg", b, jt, g][:], func=ACT.Exp,
+                                 bias=neg_lse[:, 8 * b + jt:8 * b + jt + 1])
+
+        def cast(b, jt, engine="G"):
+            T["abf", b, jt] = sb.tile([P, 2 * K], BF16, name="staging", tag="staging", bufs=3, align_bytes=64)
+            dst = T["abf", b, jt][:].rearrange("p (g v e) -> p g v e", g=2, e=2)
+            src = T["attn", b, jt][:].rearrange("p (g e v) -> p g v e", g=2, e=2)
+            if engine == "G":
+                nc.gpsimd.tensor_scalar(out=dst, in0=src, scalar1=1.0, scalar2=0.0, op0=ALU.mult, op1=ALU.add)
+            else:
+                copy(engine, dst, src)
+
+        def aw_tr(b, jt):
+            bank = sc_bank(("aw", b, jt))
+            words = T["abf", b, jt][:].bitcast(F32)
+            for s in range(4):
+                nc.tensor.transpose(bank[:, s * P:(s + 1) * P], words[:, s * P:(s + 1) * P], ident32[:])
+
+        def aw_ev(b, jt):
+            h = jt // 4
+            if jt % 4 == 0:
+                T["ai", b, h] = sb.tile([P, 8 * K], BF16, name="wide", tag="wide", bufs=3, align_bytes=64)
+            words = T["ai", b, h][:].bitcast(F32).rearrange("p (g j u) -> p g j u", g=2, u=2)
+            j0 = (jt % 4) * P
+            nc.scalar.copy(out=words[:, :, j0:j0 + P, :],
+                           in_=T["aw", b, jt][:].rearrange("p (g u j) -> p g j u", g=2, u=2))
+
+        def attn_q(b, h):
+            mx_tiles(("aq", b, h), 2 * K, "mov", MOV_BUFS)
+            quantize(("aq", b, h), T["ai", b, h][:], E4M3, slice(0, 2 * K))
+
+        def dattn(b, jt, g):
+            T["da", b, jt, g] = ps.tile([P, K], F32, name="da", tag="da", bufs=DA_BANKS)
+            j0 = (jt % 4) * P
+            mx(T["da", b, jt, g][:], ("gq", b, jt // 4), E4M3, slice(j0, j0 + P), ("dyb", b, g), E5M2, slice(0, K), True, True)
+
+        def col_sum(b, jt, g):
+            if g == 0:
+                T["part", b, jt] = sb.tile([P, 2], F32, name="part", tag="part", bufs=4)
+            prod = sb.tile([P, K], F32, name="prod", tag="prod", bufs=1)
+            nc.vector.scalar_tensor_tensor(out=prod[:], in0=T["da", b, jt, g][:], scalar=1.0,
+                                           in1=T["attn", b, jt][:, g * K:(g + 1) * K], op0=ALU.mult, op1=ALU.mult,
+                                           accum_out=T["part", b, jt][:, g:g + 1])
+
+        def col_total(b, jt):
+            T["tot", b, jt] = sb.tile([P, 1], F32, name="tot", tag="tot", bufs=4)
+            nc.vector.tensor_reduce(out=T["tot", b, jt][:], in_=T["part", b, jt][:], axis=mybir.AxisListType.X, op=ALU.add)
+
+        def dsoft(b, jt, g):
+            half = T["attn", b, jt][:, g * K:(g + 1) * K]
+            nc.vector.scalar_tensor_tensor(out=half, in0=T["da", b, jt, g][:], scalar=T["tot", b, jt][:], in1=half,
+                                           op0=ALU.subtract, op1=ALU.mult)
+
+        def o0_tr(jt, g, batch=range(B)):
+            bank = sc_bank(("o0", jt, g)) if 0 in batch else T["o0", jt, g]
+            for b in batch:
+                for n in range(4):
+                    src = g * K + n * P
+                    nc.tensor.matmul(bank[:, n * P:(n + 1) * P], lhsT=T["attn", b, jt][:, src:src + P], rhs=ident32[:],
+                                     start=(b == 0 and n == 0), stop=(b == B - 1 and n == 3), is_transpose=True)
+
+        def o0_ev(jt, g):
+            first, count = OUT0_RUNS[jt]
+            if jt == first:
+                T["o0s", g] = sb.tile([P, 4 * count * P], F32, name="raw", tag="raw", bufs=RAW_BUFS, align_bytes=64)
+            stage = T["o0s", g][:].rearrange("p (u e j) -> p u e j", u=2, e=2)
+            j0 = (jt - first) * P
+            nc.scalar.copy(out=stage[:, :, :, j0:j0 + P], in_=T["o0", jt, g][:].rearrange("p (e u j) -> p u e j", e=2, u=2))
+            if jt == first + count - 1:
+                dst = out_0[0, g * K:(g + 1) * K, first * P:(jt + 1) * P].rearrange("(p t) j -> p t j", t=4)
+                nc.sync.dma_start(out=dst, in_=rows4(T["o0s", g][:]))
+
+        def dg_mm(b, h, a):
+            bank = sc_bank(("dg", b, h, a))
+            for g in range(2):
+                mx(bank[:], ("dya", b, g), E5M2, slice(a * P, (a + 1) * P), ("aq", b, h), E4M3, slice(g * K, (g + 1) * K), g == 0, g == 1)
+
+        def dg_ev(b, h, a):
+            if a % 2 == 0:
+                T["dgs"] = sb.tile([P, 2 * K], F32, name="raw", tag="raw", bufs=RAW_BUFS, align_bytes=64)
+            nc.scalar.copy(out=T["dgs"][:, (a % 2) * K:(a % 2 + 1) * K], in_=T["dg", b, h, a][:])
+            if a % 2 == 1:
+                dst = out_1[b, :, h * K:(h + 1) * K].rearrange("(m a) j -> m a j", a=4)
+                nc.sync.dma_start(out=dst[:, a - 1:a + 1, :], in_=T["dgs"][:].rearrange("p (a j) -> p a j", a=2))
+
+        ident32 = sb.tile([P, P], F32, name="ident32")
+        ident16 = sb.tile([P, P], BF16, name="ident16")
+        lse_rows = sb.tile([P, P], F32, name="lse_rows")
+        neg_lse = sb.tile([P, 16], F32, name="neg_lse")
+        warm = sb.tile([P, 1], F32, name="warm")
+        nc.gpsimd.memset(lse_rows[:], 0.0)
+        nc.scalar.activation(out=warm[:], in_=lse_rows[:, 0:1], func=ACT.Exp)
+        make_identity(nc, ident32[:])
+        make_identity(nc, ident16[:])
+
+        def lse_load():
+            nc.sync.dma_start(out=lse_rows[0:16, :], in_=lse.rearrange("b (r p) -> (b r) p", p=P))
+
+        def lse_turn():
+            bank = sc_bank("lse")
+            nc.tensor.transpose(bank[:, 0:P], lse_rows[:], ident32[:])
+            nc.vector.tensor_scalar(out=neg_lse[:], in0=bank[:, 0:16], scalar1=-1.0, scalar2=None, op0=ALU.mult)
+
+        steps = [(b, jt) for jt in range(8) for b in range(B)]
+
+        def u_dy(b, g):
+            for a in range(4):
+                dy_mm(b, g, a); dy_ev(b, g, a)
+
+        def u_dya(b, g):
+            for pair in range(2):
+                dya_tr(b, g, pair); dya_ev(b, g, pair)
+
+        def u_aw(n):
+            aw_tr(*steps[n]); aw_ev(*steps[n])
+
+        PRE_D = 3
+
+        def lgs(b, g, h):
+            for jt in range(4 * h, 4 * h + 4):
+                logits(b, jt, g); exp(b, jt, g)
+
+        load_w(0); load_go(0, 0, 0); load_w(1); load_go(0, 1, 0); load_go(0, 0, 1)
+        w_il(0, "V"); load_go(0, 1, 1); lse_load()
+        go_il(0, 0, 0, "V"); w_il(1, "S")
+        load_go(1, 0, 0); load_go(1, 1, 0); load_pos(0, 0); load_qk(0, 0, 0)
+        w_q(0); go_q(0, 0, 0)
+        go_il(0, 1, 0, "V"); go_il(0, 0, 1, "S")
+        load_go(1, 0, 1); load_go(1, 1, 1); load_dec(); load_g(0); load_pos(1, 0); load_qk(0, 1, 0); load_g(1); load_qk(1, 0, 0); load_qk(1, 1, 0); load_pos(0, 1)
+        w_q(1); go_q(0, 1, 0)
+        go_il(0, 1, 1, "V")
+        u_dy(0, 0)
+        go_q(0, 0, 1); go_q(0, 1, 1)
+        lse_turn()
+        go_il(1, 0, 0, "V")
+        u_dy(0, 1)
+        go_il(1, 1, 0, "V"); go_q(1, 0, 0)
+        dyb_il(0, 0, "V"); go_q(1, 1, 0)
+        u_dya(0, 0)
+        lgs(0, 0, 0)
+        load_qk(0, 0, 1)
+        go_il(1, 0, 1, "V"); dyb_q(0, 0)
+        u_dya(0, 1)
+        dyb_il(0, 1, "V"); go_q(1, 0, 1); dya_q(0, 0)
+        u_dy(1, 0)
+        go_il(1, 1, 1, "S")
+        dyb_q(0, 1); dya_q(0, 1); g_add(0); go_q(1, 1, 1)
+        lgs(0, 1, 0)
+        load_qk(0, 1, 1)
+        g_il(0, 0, "V"); dyb_il(1, 0, "V"); g_q(0, 0)
+        u_dy(1, 1)
+        g_il(0, 1, E2); dyb_q(1, 0)
+        u_dya(1, 0)
+        g_add(1)
+        lgs(1, 0, 0)
+        load_pos(1, 1); load_qk(1, 0, 1)
+        dyb_il(1, 1, "V"); g_q(0, 1); dya_q(1, 0); g_il(1, 0, "V")
+        u_dya(1, 1)
+        lgs(1, 1, 0)
+        load_qk(1, 1, 1)
+        g_il(1, 1, "V"); g_q(1, 0); dya_q(1, 1); g_q(1, 1); dyb_q(1, 1)
+        late = [(0, jt, g) for g in range(2) for jt in range(4, 8)] + [(1, jt, g) for jt in range(4, 8) for g in range(2)]
+        for k in range(PRE):
+            logits(*late[k]); exp(*late[k])
+            if k == PRE_D:
+                dattn(0, 0, 0); dattn(0, 0, 1); dattn(1, 0, 0)
+        dg_units = [(b, h, a) for h in range(2) for b in range(B) for a in range(4)]
+        dgs = DGS
+        aq = AQ
+        done = {"late": PRE, "dg": 0, "turn": 0}
+        for k in range(3):
+            cast(*steps[k])
+        for n in range(17):
+            if n < 16:
+                col_sum(*steps[n], 0)
+            if n > 0:
+                dsoft(*steps[n - 1], 0)
+            if 0 < n < 16:
+                dattn(*steps[n], 1)
+            for k in range(dgs.get(n, 0)):
+                bb, hh, aa = dg_units[done["dg"]]
+                done["dg"] = done["dg"] + 1
+                dg_mm(bb, hh, aa); dg_ev(bb, hh, aa)
+            if 1 < n + 1 < 16:
+                dattn(*steps[n + 1], 0)
+            if n < 16:
+                col_sum(*steps[n], 1)
+            if n > 0:
+                dsoft(*steps[n - 1], 1)
+            if n < 16:
+                col_total(*steps[n])
+            if n in aq:
+                attn_q(*aq[n])
+            for k in range(LATE.get(n, 0)):
+                u = late[done["late"]]
+                done["late"] = done["late"] + 1
+                logits(*u); exp(*u)
+            for k in range(TURN.get(n, 0)):
+                m = done["turn"]
+                done["turn"] = m + 1
+                u_aw(m)
+                if m + 3 < 16:
+                    cast(*steps[m + 3])
+            if 2 <= n < 16:
+                jt, g = (n - 2) // 2, n % 2
+                o0_tr(jt, g); o0_ev(jt, g)
+            if n == 15:
+                o0_tr(7, 0, [0]); o0_tr(7, 1, [0])
+        for g in range(2):
+            o0_tr(7, g, [1]); o0_ev(7, g)

@@ -21,14 +21,19 @@ K = 512
 ATTN_BUFS = 16
 QK_BUFS = 4
 DA_BANKS = 4
-E1 = "V"
+E1 = "S"
 E2 = "V"
-PRE = 8
-LATE = {0: 2, 1: 2, 2: 1, 3: 1, 4: 1, 5: 1}
+PRE = 6
+CAST = "GGSGGSGGSGGSGGSG"
+PRE_D = 2
+E3 = "V"
+E4 = "V"
+LATE = {0: 2, 1: 2, 2: 2, 3: 2, 4: 2}
 OUT0_RUNS = [(0, 2), (0, 2), (2, 2), (2, 2), (4, 2), (4, 2), (6, 1), (7, 1)]
-DGS = {6: 1, 7: 1, 8: 1, 9: 1, 10: 1, 11: 3, 12: 2, 13: 2, 14: 2, 15: 2}
-AQ = {5: (0, 0), 6: (1, 0), 11: (0, 1), 12: (1, 1)}
-TURN = {0: 1, 1: 2, 2: 2, 3: 2, 4: 1, 7: 2, 8: 2, 9: 2, 10: 2}
+DGS = {5: 2, 6: 2, 7: 1, 8: 1, 9: 2, 10: 2, 11: 2, 12: 1, 13: 1, 14: 1, 15: 1}
+AQ = {4: (0, 0), 6: (1, 0), 9: (0, 1), 11: (1, 1)}
+TURN = {1: 2, 2: 2, 3: 1, 4: 2, 5: 1, 6: 2, 7: 2, 8: 1, 9: 2, 10: 1}
+O0S = {5: 1, 6: 1, 7: 1, 8: 2, 9: 1, 10: 1, 11: 2, 12: 2, 13: 1, 14: 1, 15: 1}
 MOV_BUFS = 3
 RAW_BUFS = 5
 
@@ -50,9 +55,9 @@ def tile_nonlocalblock_pa_v_kernel(
             return tile.rearrange("p (t n) -> p t n", t=4)
 
         def load(key, src, dtype, tag, bufs):
-            width = src.shape[1]
-            T[key] = sb.tile([P, 4 * width], dtype, name=tag, tag=tag, bufs=bufs, align_bytes=64)
-            nc.sync.dma_start(out=rows4(T[key][:]), in_=src.rearrange("(p t) n -> p t n", t=4))
+            rows, width = src.shape[0] // P, src.shape[1]
+            T[key] = sb.tile([P, rows * width], dtype, name=tag, tag=tag, bufs=bufs, align_bytes=64)
+            nc.sync.dma_start(out=T[key][:].rearrange("p (t n) -> p t n", t=rows), in_=src.rearrange("(p t) n -> p t n", t=rows))
 
         def load_w(q):
             load(("w", q), w_mask[q * K:(q + 1) * K, :], BF16, "raw", RAW_BUFS)
@@ -60,17 +65,22 @@ def tile_nonlocalblock_pa_v_kernel(
         def load_go(b, q, g):
             load(("go", b, q, g), go_hbm[b, q * K:(q + 1) * K, g * K:(g + 1) * K], BF16, "raw", RAW_BUFS)
 
+        def load_go_rows(b, q):
+            load(("go", b, q), go_hbm[b, q * K:(q + 1) * K, :], BF16, "wide", 3)
+
         def load_dec():
             load("dec", dec_hbm[0], BF16, "wide", 3)
 
         def load_g(b):
             load(("g", b), g_proj[b], BF16, "wide", 3)
 
-        def load_pos(g, h):
-            load(("pos", g, h), pos_embedding[0, g * K:(g + 1) * K, h * K:(h + 1) * K], BF16, "pos", 3)
+        def load_pos(g):
+            for r in range(2):
+                load(("pos", g, r), pos_embedding[0, g * K + r * 2 * P:g * K + (r + 1) * 2 * P, :], BF16, "pos", 4)
 
-        def load_qk(b, g, h):
-            load(("qk", b, g, h), qk[b, g * K:(g + 1) * K, h * K:(h + 1) * K], F32, "qk", QK_BUFS)
+        def load_qk(b, g):
+            for r in range(2):
+                load(("qk", b, g, r), qk[b, g * K + r * 2 * P:g * K + (r + 1) * 2 * P, :], F32, "qk", QK_BUFS)
 
         def copy(engine, out, in_):
             if engine == "V":
@@ -107,15 +117,16 @@ def tile_nonlocalblock_pa_v_kernel(
 
         def w_il(q, engine):
             dst = staging(("wi", q))
-            copy(engine, dst[:].rearrange("p (a m t) -> p m t a", a=4, t=4),
-                 T["w", q][:].rearrange("p (t m a) -> p m t a", t=4, a=4))
+            copy(engine, dst[:].rearrange("p (a m t) -> p a m t", a=4, t=4),
+                 T["w", q][:].rearrange("p (t m a) -> p a m t", t=4, a=4))
 
         def w_q(q):
             mx_tiles(("wq", q), K, "wq", 2)
             quantize(("wq", q), T["wi", q][:], E4M3)
 
         def go_il(b, q, g, engine):
-            interleave(engine, ("goi", b, q, g), rows4(T["go", b, q, g][:]))
+            src = rows4(T["go", b, q, g][:]) if b == 0 else rows4(T["go", b, q][:])[:, :, g * K:(g + 1) * K]
+            interleave(engine, ("goi", b, q, g), src)
 
         def go_q(b, q, g):
             if q == 0:
@@ -130,13 +141,11 @@ def tile_nonlocalblock_pa_v_kernel(
         def dy_ev(b, g, a):
             if a == 0:
                 T["dyt", b, g] = sb.tile([P, 4 * K], BF16, name="dyt", tag="dyt", bufs=2, align_bytes=64)
-            nc.scalar.copy(out=T["dyt", b, g][:, a * K:(a + 1) * K].rearrange("p (u w e) -> p u w e", u=2, e=2),
-                           in_=T["dyp", b, g, a][:].rearrange("p (w u e) -> p u w e", u=2, e=2))
+            nc.scalar.copy(out=T["dyt", b, g][:, a * K:(a + 1) * K].rearrange("p (u v) -> p u v", u=2),
+                           in_=T["dyp", b, g, a][:].rearrange("p (v u) -> p u v", u=2))
 
         def dyb_il(b, g, engine):
-            dst = staging(("dybi", b, g))
-            copy(engine, dst[:].rearrange("p (e v a) -> p v a e", e=2, a=4),
-                 T["dyt", b, g][:].rearrange("p (a v e) -> p v a e", a=4, e=2))
+            interleave(engine, ("dybi", b, g), rows4(T["dyt", b, g][:]))
 
         def dyb_q(b, g):
             mx_tiles(("dyb", b, g), K, "dyb", 4)
@@ -172,14 +181,13 @@ def tile_nonlocalblock_pa_v_kernel(
 
         def logits(b, jt, g):
             bank = sc_bank(("lg", b, jt, g))
-            h, j0 = jt // 4, (jt % 4) * P
             for n in range(4):
-                t = 2 * (n % 2) + n // 2
-                nc.tensor.matmul(bank[:, n * P:(n + 1) * P], lhsT=T["pos", g, h][:, t * K + j0:t * K + j0 + P],
+                src = (n // 2) * N + jt * P
+                nc.tensor.matmul(bank[:, n * P:(n + 1) * P], lhsT=T["pos", g, n % 2][:, src:src + P],
                                  rhs=ident16[:], start=(n == 0), stop=False)
             for n in range(4):
-                t = 2 * (n % 2) + n // 2
-                nc.tensor.matmul(bank[:, n * P:(n + 1) * P], lhsT=T["qk", b, g, h][:, t * K + j0:t * K + j0 + P],
+                src = (n // 2) * N + jt * P
+                nc.tensor.matmul(bank[:, n * P:(n + 1) * P], lhsT=T["qk", b, g, n % 2][:, src:src + P],
                                  rhs=ident32[:], start=False, stop=(n == 3), is_transpose=True)
 
         def exp(b, jt, g):
@@ -190,8 +198,8 @@ def tile_nonlocalblock_pa_v_kernel(
 
         def cast(b, jt, engine="G"):
             T["abf", b, jt] = sb.tile([P, 2 * K], BF16, name="staging", tag="staging", bufs=3, align_bytes=64)
-            dst = T["abf", b, jt][:].rearrange("p (g v e) -> p g v e", g=2, e=2)
-            src = T["attn", b, jt][:].rearrange("p (g e v) -> p g v e", g=2, e=2)
+            dst = T["abf", b, jt][:]
+            src = T["attn", b, jt][:]
             if engine == "G":
                 nc.gpsimd.tensor_scalar(out=dst, in0=src, scalar1=1.0, scalar2=0.0, op0=ALU.mult, op1=ALU.add)
             else:
@@ -250,12 +258,14 @@ def tile_nonlocalblock_pa_v_kernel(
             first, count = OUT0_RUNS[jt]
             if jt == first:
                 T["o0s", g] = sb.tile([P, 4 * count * P], F32, name="raw", tag="raw", bufs=RAW_BUFS, align_bytes=64)
-            stage = T["o0s", g][:].rearrange("p (u e j) -> p u e j", u=2, e=2)
+            stage = T["o0s", g][:].rearrange("p (r u j) -> p r u j", r=2, u=2)
             j0 = (jt - first) * P
-            nc.scalar.copy(out=stage[:, :, :, j0:j0 + P], in_=T["o0", jt, g][:].rearrange("p (e u j) -> p u e j", e=2, u=2))
+            nc.scalar.copy(out=stage[:, :, :, j0:j0 + P], in_=T["o0", jt, g][:].rearrange("p (u r j) -> p r u j", u=2, r=2))
             if jt == first + count - 1:
-                dst = out_0[0, g * K:(g + 1) * K, first * P:(jt + 1) * P].rearrange("(p t) j -> p t j", t=4)
-                nc.sync.dma_start(out=dst, in_=rows4(T["o0s", g][:]))
+                for r in range(2):
+                    i0 = g * K + r * 2 * P
+                    dst = out_0[0, i0:i0 + 2 * P, first * P:(jt + 1) * P].rearrange("(p u) j -> p u j", u=2)
+                    nc.sync.dma_start(out=dst, in_=stage[:, r, :, :])
 
         def dg_mm(b, h, a):
             bank = sc_bank(("dg", b, h, a))
@@ -288,7 +298,8 @@ def tile_nonlocalblock_pa_v_kernel(
             nc.tensor.transpose(bank[:, 0:P], lse_rows[:], ident32[:])
             nc.vector.tensor_scalar(out=neg_lse[:], in0=bank[:, 0:16], scalar1=-1.0, scalar2=None, op0=ALU.mult)
 
-        steps = [(b, jt) for jt in range(8) for b in range(B)]
+        steps = [(b, jt) for b in range(B) for jt in range(4)] + [(b, jt) for jt in range(4, 8) for b in range(B)]
+        tiles = [(b, jt) for h in range(2) for b in range(B) for jt in range(4 * h, 4 * h + 4)]
 
         def u_dy(b, g):
             for a in range(4):
@@ -299,21 +310,18 @@ def tile_nonlocalblock_pa_v_kernel(
                 dya_tr(b, g, pair); dya_ev(b, g, pair)
 
         def u_aw(n):
-            aw_tr(*steps[n]); aw_ev(*steps[n])
+            aw_tr(*tiles[n]); aw_ev(*tiles[n])
 
-        PRE_D = 3
-
-        def lgs(b, g, h):
-            for jt in range(4 * h, 4 * h + 4):
+        def lgs(b, g, lo=0, hi=8):
+            for jt in range(lo, hi):
                 logits(b, jt, g); exp(b, jt, g)
 
         load_w(0); load_go(0, 0, 0); load_w(1); load_go(0, 1, 0); load_go(0, 0, 1)
         w_il(0, "V"); load_go(0, 1, 1); lse_load()
+        load_go_rows(1, 0); load_go_rows(1, 1); load_pos(0); load_qk(0, 0); load_dec()
         go_il(0, 0, 0, "V"); w_il(1, "S")
-        load_go(1, 0, 0); load_go(1, 1, 0); load_pos(0, 0); load_qk(0, 0, 0)
         w_q(0); go_q(0, 0, 0)
         go_il(0, 1, 0, "V"); go_il(0, 0, 1, "S")
-        load_go(1, 0, 1); load_go(1, 1, 1); load_dec(); load_g(0); load_pos(1, 0); load_qk(0, 1, 0); load_g(1); load_qk(1, 0, 0); load_qk(1, 1, 0); load_pos(0, 1)
         w_q(1); go_q(0, 1, 0)
         go_il(0, 1, 1, "V")
         u_dy(0, 0)
@@ -322,49 +330,47 @@ def tile_nonlocalblock_pa_v_kernel(
         go_il(1, 0, 0, "V")
         u_dy(0, 1)
         go_il(1, 1, 0, "V"); go_q(1, 0, 0)
-        dyb_il(0, 0, "V"); go_q(1, 1, 0)
+        go_il(1, 0, 1, "V"); go_q(1, 1, 0)
+        load_g(0); load_pos(1); load_qk(0, 1)
         u_dya(0, 0)
-        lgs(0, 0, 0)
-        load_qk(0, 0, 1)
-        go_il(1, 0, 1, "V"); dyb_q(0, 0)
         u_dya(0, 1)
-        dyb_il(0, 1, "V"); go_q(1, 0, 1); dya_q(0, 0)
+        go_il(1, 1, 1, E1)
+        load_g(1)
+        dyb_il(0, 0, "V"); go_q(1, 0, 1)
         u_dy(1, 0)
-        go_il(1, 1, 1, "S")
-        dyb_q(0, 1); dya_q(0, 1); g_add(0); go_q(1, 1, 1)
-        lgs(0, 1, 0)
-        load_qk(0, 1, 1)
-        g_il(0, 0, "V"); dyb_il(1, 0, "V"); g_q(0, 0)
+        dyb_il(0, 1, "V"); go_q(1, 1, 1); dyb_q(0, 0); dya_q(0, 0); dyb_q(0, 1); dya_q(0, 1)
         u_dy(1, 1)
-        g_il(0, 1, E2); dyb_q(1, 0)
+        dyb_il(1, 0, "V")
         u_dya(1, 0)
-        g_add(1)
-        lgs(1, 0, 0)
-        load_pos(1, 1); load_qk(1, 0, 1)
-        dyb_il(1, 1, "V"); g_q(0, 1); dya_q(1, 0); g_il(1, 0, "V")
+        g_add(0); dyb_q(1, 0)
+        lgs(0, 0)
+        load_qk(1, 0)
         u_dya(1, 1)
-        lgs(1, 1, 0)
-        load_qk(1, 1, 1)
-        g_il(1, 1, "V"); g_q(1, 0); dya_q(1, 1); g_q(1, 1); dyb_q(1, 1)
-        late = [(0, jt, g) for g in range(2) for jt in range(4, 8)] + [(1, jt, g) for jt in range(4, 8) for g in range(2)]
+        g_il(0, 0, "V"); dya_q(1, 0); g_il(0, 1, E2); g_q(0, 0)
+        lgs(0, 1)
+        load_qk(1, 1)
+        dyb_il(1, 1, "V"); g_q(0, 1); dya_q(1, 1); g_add(1); g_il(1, 0, "V"); g_il(1, 1, E3)
+        dattn(0, 0, 0); dattn(0, 0, 1); dattn(0, 1, 0)
+        g_q(1, 0); g_q(1, 1); dyb_q(1, 1)
+        late = [(1, jt, 0) for jt in range(PRE)]
+        late = late + [u for u in [(1, jt, g) for jt in range(8) for g in range(2)] if u not in late]
         for k in range(PRE):
             logits(*late[k]); exp(*late[k])
-            if k == PRE_D:
-                dattn(0, 0, 0); dattn(0, 0, 1); dattn(1, 0, 0)
         dg_units = [(b, h, a) for h in range(2) for b in range(B) for a in range(4)]
-        dgs = DGS
-        aq = AQ
-        done = {"late": PRE, "dg": 0, "turn": 0}
+        o0_units = [(jt, g) for jt in range(8) for g in range(2)]
+        done = {"late": PRE, "dg": 0, "turn": 0, "o0": 0}
         for k in range(3):
-            cast(*steps[k])
+            cast(*tiles[k], CAST[k])
         for n in range(17):
             if n < 16:
                 col_sum(*steps[n], 0)
             if n > 0:
                 dsoft(*steps[n - 1], 0)
+            if n in AQ:
+                attn_q(*AQ[n])
             if 0 < n < 16:
                 dattn(*steps[n], 1)
-            for k in range(dgs.get(n, 0)):
+            for k in range(DGS.get(n, 0)):
                 bb, hh, aa = dg_units[done["dg"]]
                 done["dg"] = done["dg"] + 1
                 dg_mm(bb, hh, aa); dg_ev(bb, hh, aa)
@@ -376,20 +382,19 @@ def tile_nonlocalblock_pa_v_kernel(
                 dsoft(*steps[n - 1], 1)
             if n < 16:
                 col_total(*steps[n])
-            if n in aq:
-                attn_q(*aq[n])
+            for k in range(TURN.get(n, 0)):
+                u_aw(done["turn"])
+                done["turn"] = done["turn"] + 1
             for k in range(LATE.get(n, 0)):
                 u = late[done["late"]]
                 done["late"] = done["late"] + 1
                 logits(*u); exp(*u)
-            for k in range(TURN.get(n, 0)):
-                m = done["turn"]
-                done["turn"] = m + 1
-                u_aw(m)
+            for m in range(done["turn"] - TURN.get(n, 0), done["turn"]):
                 if m + 3 < 16:
-                    cast(*steps[m + 3])
-            if 2 <= n < 16:
-                jt, g = (n - 2) // 2, n % 2
+                    cast(*tiles[m + 3], CAST[m + 3])
+            for k in range(O0S.get(n, 0)):
+                jt, g = o0_units[done["o0"]]
+                done["o0"] = done["o0"] + 1
                 o0_tr(jt, g); o0_ev(jt, g)
             if n == 15:
                 o0_tr(7, 0, [0]); o0_tr(7, 1, [0])

@@ -18,24 +18,24 @@ ACT = mybir.ActivationFunctionType
 
 P = 128
 K = 512
-ATTN_BUFS = 16
-QK_BUFS = 4
-DA_BANKS = 4
-E1 = "S"
-E2 = "V"
-PRE = 6
-CAST = "GGSGGSGGSGGSGGSG"
-PRE_D = 2
-E3 = "V"
-E4 = "V"
-LATE = {0: 2, 1: 2, 2: 2, 3: 2, 4: 2}
-OUT0_RUNS = [(0, 2), (0, 2), (2, 2), (2, 2), (4, 2), (4, 2), (6, 1), (7, 1)]
-DGS = {5: 2, 6: 2, 7: 1, 8: 1, 9: 2, 10: 2, 11: 2, 12: 1, 13: 1, 14: 1, 15: 1}
-AQ = {4: (0, 0), 6: (1, 0), 9: (0, 1), 11: (1, 1)}
-TURN = {1: 2, 2: 2, 3: 1, 4: 2, 5: 1, 6: 2, 7: 2, 8: 1, 9: 2, 10: 1}
-O0S = {5: 1, 6: 1, 7: 1, 8: 2, 9: 1, 10: 1, 11: 2, 12: 2, 13: 1, 14: 1, 15: 1}
-MOV_BUFS = 3
-RAW_BUFS = 5
+TILES = N // P
+STEPS = B * TILES
+
+SMALL_BUFS = 5
+WIDE_BUFS = 4
+QK_BUFS = 5
+STAGING_BUFS = 3
+MOVING_BUFS = 3
+DATTN_BANKS = 4
+SCALAR_BANKS = 8 - DATTN_BANKS
+
+LOGIT_BATCH = 2
+EARLY_LOGITS = 6
+SIDE_UNITS = 3
+SCALAR_ROUNDS = 3
+TURNS_OF_A_HALF = (2, 2, 1, 2, 1)
+GPSIMD_SUMS = range(TILES // 2, TILES - 1)
+OUT0_RUNS = [(jt - jt % 2, 2) for jt in range(TILES - 2)] + [(TILES - 2, 1), (TILES - 1, 1)]
 
 
 def tile_nonlocalblock_pa_v_kernel(
@@ -49,354 +49,391 @@ def tile_nonlocalblock_pa_v_kernel(
         sb = ctx.enter_context(tc.tile_pool(name="sb", bufs=1))
         ps = ctx.enter_context(tc.psum_pool(name="ps", bufs=1))
         ctx.enter_context(tc.manual_schedule())
-        T = {}
 
-        def rows4(tile):
-            return tile.rearrange("p (t n) -> p t n", t=4)
+        made = {}
+
+        def span(k, width):
+            return slice(k * width, (k + 1) * width)
+
+        def four_rows(ap):
+            return ap.rearrange("p (t n) -> p t n", t=4)
+
+        def sbuf(key, width, dtype, tag, bufs):
+            made[key] = sb.tile([P, width], dtype, name=tag, tag=tag, bufs=bufs, align_bytes=64)
+            return made[key]
+
+        def scalar_bank(key):
+            made[key] = ps.tile([P, K], F32, name="scalar_bank", tag="scalar_bank", bufs=SCALAR_BANKS)
+            return made[key]
 
         def load(key, src, dtype, tag, bufs):
             rows, width = src.shape[0] // P, src.shape[1]
-            T[key] = sb.tile([P, rows * width], dtype, name=tag, tag=tag, bufs=bufs, align_bytes=64)
-            nc.sync.dma_start(out=T[key][:].rearrange("p (t n) -> p t n", t=rows), in_=src.rearrange("(p t) n -> p t n", t=rows))
+            tile = sbuf(key, rows * width, dtype, tag, bufs)
+            nc.sync.dma_start(out=tile[:].rearrange("p (t n) -> p t n", t=rows),
+                              in_=src.rearrange("(p t) n -> p t n", t=rows))
 
         def load_w(q):
-            load(("w", q), w_mask[q * K:(q + 1) * K, :], BF16, "raw", RAW_BUFS)
+            load(("w", q), w_mask[span(q, K), :], BF16, "small", SMALL_BUFS)
 
-        def load_go(b, q, g):
-            load(("go", b, q, g), go_hbm[b, q * K:(q + 1) * K, g * K:(g + 1) * K], BF16, "raw", RAW_BUFS)
+        def load_go_group(q, s):
+            load(("go", 0, q, s), go_hbm[0, span(q, K), span(s, K)], BF16, "small", SMALL_BUFS)
 
-        def load_go_rows(b, q):
-            load(("go", b, q), go_hbm[b, q * K:(q + 1) * K, :], BF16, "wide", 3)
+        def load_go_rows(q):
+            load(("go", 1, q), go_hbm[1, span(q, K), :], BF16, "wide", WIDE_BUFS)
 
         def load_dec():
-            load("dec", dec_hbm[0], BF16, "wide", 3)
+            load("dec", dec_hbm[0], BF16, "wide", WIDE_BUFS)
 
         def load_g(b):
-            load(("g", b), g_proj[b], BF16, "wide", 3)
+            load(("g", b), g_proj[b], BF16, "wide", WIDE_BUFS)
 
-        def load_pos(g):
+        def load_pos(s):
             for r in range(2):
-                load(("pos", g, r), pos_embedding[0, g * K + r * 2 * P:g * K + (r + 1) * 2 * P, :], BF16, "pos", 4)
+                load(("pos", s, r), pos_embedding[0, span(2 * s + r, 2 * P), :], BF16, "pos", 4)
 
-        def load_qk(b, g):
-            for r in range(2):
-                load(("qk", b, g, r), qk[b, g * K + r * 2 * P:g * K + (r + 1) * 2 * P, :], F32, "qk", QK_BUFS)
+        def load_qk(b, s, r):
+            load(("qk", b, s, r), qk[b, span(2 * s + r, 2 * P), :], F32, "qk", QK_BUFS)
 
-        def copy(engine, out, in_):
-            if engine == "V":
-                nc.vector.tensor_copy(out=out, in_=in_)
-            else:
-                nc.scalar.copy(out=out, in_=in_)
+        def load_lse():
+            nc.sync.dma_start(out=lse_rows[0:STEPS, :], in_=lse.rearrange("b (jt p) -> (b jt) p", p=P))
 
-        def staging(key):
-            T[key] = sb.tile([P, 4 * K], BF16, name="staging", tag="staging", bufs=3, align_bytes=64)
-            return T[key]
+        def on_vector(out, in_):
+            nc.vector.tensor_copy(out=out, in_=in_)
 
-        def mx_tiles(key, width, tag, bufs):
+        def on_scalar(out, in_):
+            nc.scalar.copy(out=out, in_=in_)
+
+        def on_gpsimd(out, in_):
+            nc.gpsimd.tensor_scalar(out=out, in0=in_, scalar1=1.0, scalar2=0.0, op0=ALU.mult, op1=ALU.add)
+
+        def interleave(copy, key, src):
+            tile = sbuf(key, 4 * K, BF16, "staging", STAGING_BUFS)
+            copy(tile[:].rearrange("p (n k t) -> p n t k", k=4, t=4), src.rearrange("p t (n k) -> p n t k", k=4))
+
+        def operand(key, fmt, width, tag, bufs):
             codes = sb.tile([P, width], U32, name=tag + "_codes", tag=tag + "_codes", bufs=bufs, align_bytes=64)
             scales = sb.tile([P, width], U8, name=tag + "_scales", tag=tag + "_scales", bufs=bufs, align_bytes=64)
-            T[key] = (codes, scales)
+            made[key] = (codes, scales, fmt)
 
-        def quantize(key, src, fmt, cols=slice(0, K)):
-            codes, scales = T[key]
-            nc.vector.quantize_mx(out=codes[:, cols].bitcast(fmt), scales=scales[:, cols], in_=src)
+        def quantize(key, cols, src):
+            codes, scales, fmt = made[key]
+            nc.vector.quantize_mx(out=codes[:, cols].bitcast(fmt), scales=scales[:, cols], in_=src[:])
 
-        def mx(out, lhs_key, lhs_fmt, lhs_cols, rhs_key, rhs_fmt, rhs_cols, start, stop):
-            lc, lsc = T[lhs_key]
-            rc, rsc = T[rhs_key]
-            nc.tensor.matmul_mx(out=out, lhsT=lc[:, lhs_cols].bitcast(lhs_fmt), lhsT_scale=lsc[:, lhs_cols],
-                                rhs=rc[:, rhs_cols].bitcast(rhs_fmt), rhs_scale=rsc[:, rhs_cols], start=start, stop=stop)
+        def product(out, lhs_key, lhs_cols, rhs_key, rhs_cols, start, stop):
+            lhs_codes, lhs_scales, lhs_fmt = made[lhs_key]
+            rhs_codes, rhs_scales, rhs_fmt = made[rhs_key]
+            nc.tensor.matmul_mx(out=out[:], lhsT=lhs_codes[:, lhs_cols].bitcast(lhs_fmt), lhsT_scale=lhs_scales[:, lhs_cols],
+                                rhs=rhs_codes[:, rhs_cols].bitcast(rhs_fmt), rhs_scale=rhs_scales[:, rhs_cols],
+                                start=start, stop=stop)
 
-        def sc_bank(key):
-            T[key] = ps.tile([P, K], F32, name="sc", tag="sc", bufs=8 - DA_BANKS)
-            return T[key]
+        def w_interleave(q, copy):
+            tile = sbuf(("w_in", q), 4 * K, BF16, "staging", STAGING_BUFS)
+            copy(tile[:].rearrange("p (a m t) -> p a m t", a=4, t=4),
+                 made["w", q][:].rearrange("p (t m a) -> p a m t", t=4, a=4))
 
-        def interleave(engine, key, src):
-            dst = staging(key)
-            copy(engine, dst[:].rearrange("p (c i t) -> p c t i", i=4, t=4), src.rearrange("p t (c i) -> p c t i", i=4))
+        def w_quantize(q):
+            operand(("w_mx", q), E4M3, K, "w", 2)
+            quantize(("w_mx", q), span(0, K), made["w_in", q])
 
-        def w_il(q, engine):
-            dst = staging(("wi", q))
-            copy(engine, dst[:].rearrange("p (a m t) -> p a m t", a=4, t=4),
-                 T["w", q][:].rearrange("p (t m a) -> p a m t", t=4, a=4))
+        def go_interleave(b, q, s, copy):
+            src = four_rows(made["go", 0, q, s][:]) if b == 0 else four_rows(made["go", 1, q][:])[:, :, span(s, K)]
+            interleave(copy, ("go_in", b, q, s), src)
 
-        def w_q(q):
-            mx_tiles(("wq", q), K, "wq", 2)
-            quantize(("wq", q), T["wi", q][:], E4M3)
-
-        def go_il(b, q, g, engine):
-            src = rows4(T["go", b, q, g][:]) if b == 0 else rows4(T["go", b, q][:])[:, :, g * K:(g + 1) * K]
-            interleave(engine, ("goi", b, q, g), src)
-
-        def go_q(b, q, g):
+        def go_quantize(b, q, s):
             if q == 0:
-                mx_tiles(("goq", b, g), 2 * K, "mov", MOV_BUFS)
-            quantize(("goq", b, g), T["goi", b, q, g][:], E5M2, slice(q * K, (q + 1) * K))
-
-        def dy_mm(b, g, a):
-            bank = sc_bank(("dyp", b, g, a))
-            for q in range(2):
-                mx(bank[:], ("wq", q), E4M3, slice(a * P, (a + 1) * P), ("goq", b, g), E5M2, slice(q * K, (q + 1) * K), q == 0, q == 1)
-
-        def dy_ev(b, g, a):
-            if a == 0:
-                T["dyt", b, g] = sb.tile([P, 4 * K], BF16, name="dyt", tag="dyt", bufs=2, align_bytes=64)
-            nc.scalar.copy(out=T["dyt", b, g][:, a * K:(a + 1) * K].rearrange("p (u v) -> p u v", u=2),
-                           in_=T["dyp", b, g, a][:].rearrange("p (v u) -> p u v", u=2))
-
-        def dyb_il(b, g, engine):
-            interleave(engine, ("dybi", b, g), rows4(T["dyt", b, g][:]))
-
-        def dyb_q(b, g):
-            mx_tiles(("dyb", b, g), K, "dyb", 4)
-            quantize(("dyb", b, g), T["dybi", b, g][:], E5M2)
-
-        def dya_tr(b, g, pair):
-            bank = sc_bank(("dyw", b, g, pair))
-            words = T["dyt", b, g][:].bitcast(F32)
-            for s in range(4):
-                src = (4 * pair + s) * P
-                nc.tensor.transpose(bank[:, s * P:(s + 1) * P], words[:, src:src + P], ident32[:])
-
-        def dya_ev(b, g, pair):
-            if pair == 0:
-                T["dyai", b, g] = sb.tile([P, 4 * K], BF16, name="dyai", tag="dyai", bufs=2, align_bytes=64)
-            words = T["dyai", b, g][:].bitcast(F32)
-            nc.scalar.copy(out=words[:, pair * K:(pair + 1) * K].rearrange("p (a m u) -> p a m u", a=2, u=2),
-                           in_=T["dyw", b, g, pair][:].rearrange("p (a u m) -> p a m u", a=2, u=2))
-
-        def dya_q(b, g):
-            mx_tiles(("dya", b, g), K, "dya", 4)
-            quantize(("dya", b, g), T["dyai", b, g][:], E5M2)
+                operand(("go_mx", b, s), E5M2, 2 * K, "moving", MOVING_BUFS)
+            quantize(("go_mx", b, s), span(q, K), made["go_in", b, q, s])
 
         def g_add(b):
-            nc.vector.tensor_tensor(out=T["g", b][:], in0=T["g", b][:], in1=T["dec"][:], op=ALU.add)
+            nc.vector.tensor_tensor(out=made["g", b][:], in0=made["g", b][:], in1=made["dec"][:], op=ALU.add)
 
-        def g_il(b, h, engine):
-            interleave(engine, ("gi", b, h), rows4(T["g", b][:])[:, :, h * K:(h + 1) * K])
+        def g_interleave(b, h):
+            interleave(on_vector, ("g_in", b, h), four_rows(made["g", b][:])[:, :, span(h, K)])
 
-        def g_q(b, h):
-            mx_tiles(("gq", b, h), K, "gq", 4)
-            quantize(("gq", b, h), T["gi", b, h][:], E4M3)
+        def g_quantize(b, h):
+            operand(("g_mx", b, h), E4M3, K, "g", 4)
+            quantize(("g_mx", b, h), span(0, K), made["g_in", b, h])
 
-        def logits(b, jt, g):
-            bank = sc_bank(("lg", b, jt, g))
-            for n in range(4):
-                src = (n // 2) * N + jt * P
-                nc.tensor.matmul(bank[:, n * P:(n + 1) * P], lhsT=T["pos", g, n % 2][:, src:src + P],
-                                 rhs=ident16[:], start=(n == 0), stop=False)
-            for n in range(4):
-                src = (n // 2) * N + jt * P
-                nc.tensor.matmul(bank[:, n * P:(n + 1) * P], lhsT=T["qk", b, g, n % 2][:, src:src + P],
-                                 rhs=ident32[:], start=False, stop=(n == 3), is_transpose=True)
+        def dy_products(b, s):
+            for a in range(4):
+                bank = scalar_bank("dy")
+                for q in range(2):
+                    product(bank, ("w_mx", q), span(a, P), ("go_mx", b, s), span(q, K), q == 0, q == 1)
+                if a == 0:
+                    sbuf(("dy_bf", b, s), 4 * K, BF16, "small", SMALL_BUFS)
+                nc.scalar.copy(out=made["dy_bf", b, s][:, span(a, K)].rearrange("p (u v) -> p u v", u=2),
+                               in_=bank[:].rearrange("p (v u) -> p u v", u=2))
 
-        def exp(b, jt, g):
-            if g == 0:
-                T["attn", b, jt] = sb.tile([P, 2 * K], F32, name="attn", tag="attn", bufs=ATTN_BUFS, align_bytes=64)
-            nc.scalar.activation(out=T["attn", b, jt][:, g * K:(g + 1) * K], in_=T["lg", b, jt, g][:], func=ACT.Exp,
-                                 bias=neg_lse[:, 8 * b + jt:8 * b + jt + 1])
+        def dy_c_interleave(b, s):
+            interleave(on_vector, ("dy_c_in", b, s), four_rows(made["dy_bf", b, s][:]))
 
-        def cast(b, jt, engine="G"):
-            T["abf", b, jt] = sb.tile([P, 2 * K], BF16, name="staging", tag="staging", bufs=3, align_bytes=64)
-            dst = T["abf", b, jt][:]
-            src = T["attn", b, jt][:]
-            if engine == "G":
-                nc.gpsimd.tensor_scalar(out=dst, in0=src, scalar1=1.0, scalar2=0.0, op0=ALU.mult, op1=ALU.add)
-            else:
-                copy(engine, dst, src)
+        def dy_c_quantize(b, s):
+            operand(("dy_c", b, s), E5M2, K, "dy_c", 4)
+            quantize(("dy_c", b, s), span(0, K), made["dy_c_in", b, s])
 
-        def aw_tr(b, jt):
-            bank = sc_bank(("aw", b, jt))
-            words = T["abf", b, jt][:].bitcast(F32)
-            for s in range(4):
-                nc.tensor.transpose(bank[:, s * P:(s + 1) * P], words[:, s * P:(s + 1) * P], ident32[:])
+        def dy_turn(b, s):
+            words = made["dy_bf", b, s][:].bitcast(F32)
+            for pair in range(2):
+                bank = scalar_bank("dy_words")
+                for k in range(4):
+                    nc.tensor.transpose(bank[:, span(k, P)], words[:, span(4 * pair + k, P)], ident32[:])
+                if pair == 0:
+                    sbuf(("dy_i_in", b, s), 4 * K, BF16, "small", SMALL_BUFS)
+                dst = made["dy_i_in", b, s][:].bitcast(F32)[:, span(pair, K)]
+                nc.scalar.copy(out=dst.rearrange("p (a m u) -> p a m u", a=2, u=2),
+                               in_=bank[:].rearrange("p (a u m) -> p a m u", a=2, u=2))
 
-        def aw_ev(b, jt):
-            h = jt // 4
+        def dy_i_quantize(b, s):
+            operand(("dy_i", b, s), E5M2, K, "dy_i", 4)
+            quantize(("dy_i", b, s), span(0, K), made["dy_i_in", b, s])
+
+        def lse_turn():
+            bank = scalar_bank("lse")
+            nc.tensor.transpose(bank[:, 0:P], lse_rows[:], ident32[:])
+            nc.scalar.activation(out=neg_lse[:], in_=bank[:, 0:STEPS], func=ACT.Identity, scale=-1.0)
+
+        def logit_blocks(kind, jt):
+            return [made[kind + (k % 2,)][:, span(TILES * (k // 2) + jt, P)] for k in range(4)]
+
+        def probabilities(units):
+            for b, jt, s in units:
+                bank = scalar_bank(("logits", b, jt, s))
+                for k, block in enumerate(logit_blocks(("pos", s), jt)):
+                    nc.tensor.matmul(bank[:, span(k, P)], lhsT=block, rhs=ident16[:], start=(k == 0), stop=False)
+            for b, jt, s in units:
+                bank = made["logits", b, jt, s]
+                for k, block in enumerate(logit_blocks(("qk", b, s), jt)):
+                    nc.tensor.matmul(bank[:, span(k, P)], lhsT=block, rhs=ident32[:], start=False, stop=(k == 3),
+                                     is_transpose=True)
+                if s == 0:
+                    sbuf(("attn", b, jt), N, F32, "attn", STEPS)
+                nc.scalar.activation(out=made["attn", b, jt][:, span(s, K)], in_=bank[:], func=ACT.Exp,
+                                     bias=neg_lse[:, span(TILES * b + jt, 1)])
+
+        def probabilities_in_batches(units):
+            for k in range(0, len(units), LOGIT_BATCH):
+                probabilities(units[k:k + LOGIT_BATCH])
+
+        def attn_round(b, jt, copy):
+            copy(sbuf(("attn_bf", b, jt), N, BF16, "staging", STAGING_BUFS)[:], made["attn", b, jt][:])
+
+        def attn_turn(b, jt):
+            bank = scalar_bank("attn_words")
+            words = made["attn_bf", b, jt][:].bitcast(F32)
+            for k in range(4):
+                nc.tensor.transpose(bank[:, span(k, P)], words[:, span(k, P)], ident32[:])
             if jt % 4 == 0:
-                T["ai", b, h] = sb.tile([P, 8 * K], BF16, name="wide", tag="wide", bufs=3, align_bytes=64)
-            words = T["ai", b, h][:].bitcast(F32).rearrange("p (g j u) -> p g j u", g=2, u=2)
-            j0 = (jt % 4) * P
-            nc.scalar.copy(out=words[:, :, j0:j0 + P, :],
-                           in_=T["aw", b, jt][:].rearrange("p (g u j) -> p g j u", g=2, u=2))
+                sbuf(("attn_in", b, jt // 4), 8 * K, BF16, "wide", WIDE_BUFS)
+            dst = made["attn_in", b, jt // 4][:].bitcast(F32).rearrange("p (s j u) -> p s j u", s=2, u=2)
+            nc.scalar.copy(out=dst[:, :, span(jt % 4, P), :], in_=bank[:].rearrange("p (s u j) -> p s j u", s=2, u=2))
 
-        def attn_q(b, h):
-            mx_tiles(("aq", b, h), 2 * K, "mov", MOV_BUFS)
-            quantize(("aq", b, h), T["ai", b, h][:], E4M3, slice(0, 2 * K))
+        def attn_quantize(b, h):
+            operand(("attn_mx", b, h), E4M3, 2 * K, "moving", MOVING_BUFS)
+            quantize(("attn_mx", b, h), span(0, 2 * K), made["attn_in", b, h])
 
-        def dattn(b, jt, g):
-            T["da", b, jt, g] = ps.tile([P, K], F32, name="da", tag="da", bufs=DA_BANKS)
-            j0 = (jt % 4) * P
-            mx(T["da", b, jt, g][:], ("gq", b, jt // 4), E4M3, slice(j0, j0 + P), ("dyb", b, g), E5M2, slice(0, K), True, True)
+        def dattn(b, jt, s):
+            made["dattn", b, jt, s] = ps.tile([P, K], F32, name="dattn", tag="dattn", bufs=DATTN_BANKS)
+            product(made["dattn", b, jt, s], ("g_mx", b, jt // 4), span(jt % 4, P), ("dy_c", b, s), span(0, K), True, True)
 
-        def col_sum(b, jt, g):
-            if g == 0:
-                T["part", b, jt] = sb.tile([P, 2], F32, name="part", tag="part", bufs=4)
-            prod = sb.tile([P, K], F32, name="prod", tag="prod", bufs=1)
-            nc.vector.scalar_tensor_tensor(out=prod[:], in0=T["da", b, jt, g][:], scalar=1.0,
-                                           in1=T["attn", b, jt][:, g * K:(g + 1) * K], op0=ALU.mult, op1=ALU.mult,
-                                           accum_out=T["part", b, jt][:, g:g + 1])
+        def partial_sum(b, jt, s):
+            if s == 0:
+                made["partial", b, jt] = sb.tile([P, 2], F32, name="partial", tag="partial", bufs=4)
+            products = sb.tile([P, K], F32, name="products", tag="products", bufs=1)
+            nc.vector.scalar_tensor_tensor(out=products[:], in0=made["dattn", b, jt, s][:], scalar=1.0,
+                                           in1=made["attn", b, jt][:, span(s, K)], op0=ALU.mult, op1=ALU.mult,
+                                           accum_out=made["partial", b, jt][:, span(s, 1)])
 
-        def col_total(b, jt):
-            T["tot", b, jt] = sb.tile([P, 1], F32, name="tot", tag="tot", bufs=4)
-            nc.vector.tensor_reduce(out=T["tot", b, jt][:], in_=T["part", b, jt][:], axis=mybir.AxisListType.X, op=ALU.add)
+        def total_sum(b, jt):
+            made["total", b, jt] = sb.tile([P, 1], F32, name="total", tag="total", bufs=4)
+            nc.vector.tensor_reduce(out=made["total", b, jt][:], in_=made["partial", b, jt][:],
+                                    axis=mybir.AxisListType.X, op=ALU.add)
 
-        def dsoft(b, jt, g):
-            half = T["attn", b, jt][:, g * K:(g + 1) * K]
-            nc.vector.scalar_tensor_tensor(out=half, in0=T["da", b, jt, g][:], scalar=T["tot", b, jt][:], in1=half,
-                                           op0=ALU.subtract, op1=ALU.mult)
+        def ds(b, jt, s):
+            half = made["attn", b, jt][:, span(s, K)]
+            nc.vector.scalar_tensor_tensor(out=half, in0=made["dattn", b, jt, s][:], scalar=made["total", b, jt][:],
+                                           in1=half, op0=ALU.subtract, op1=ALU.mult)
+            if b == B - 1 and jt in GPSIMD_SUMS:
+                nc.gpsimd.tensor_tensor(out=half, in0=half, in1=made["attn", 0, jt][:, span(s, K)], op=ALU.add)
 
-        def o0_tr(jt, g, batch=range(B)):
-            bank = sc_bank(("o0", jt, g)) if 0 in batch else T["o0", jt, g]
-            for b in batch:
-                for n in range(4):
-                    src = g * K + n * P
-                    nc.tensor.matmul(bank[:, n * P:(n + 1) * P], lhsT=T["attn", b, jt][:, src:src + P], rhs=ident32[:],
-                                     start=(b == 0 and n == 0), stop=(b == B - 1 and n == 3), is_transpose=True)
+        def out0_turn(jt, s, b):
+            opens = b == 0 or jt in GPSIMD_SUMS
+            bank = scalar_bank(("out0", jt, s)) if opens else made["out0", jt, s]
+            for k in range(4):
+                nc.tensor.matmul(bank[:, span(k, P)], lhsT=made["attn", b, jt][:, span(4 * s + k, P)], rhs=ident32[:],
+                                 start=(opens and k == 0), stop=(b == B - 1 and k == 3), is_transpose=True)
 
-        def o0_ev(jt, g):
+        def out0_store(jt, s):
             first, count = OUT0_RUNS[jt]
             if jt == first:
-                T["o0s", g] = sb.tile([P, 4 * count * P], F32, name="raw", tag="raw", bufs=RAW_BUFS, align_bytes=64)
-            stage = T["o0s", g][:].rearrange("p (r u j) -> p r u j", r=2, u=2)
-            j0 = (jt - first) * P
-            nc.scalar.copy(out=stage[:, :, :, j0:j0 + P], in_=T["o0", jt, g][:].rearrange("p (u r j) -> p r u j", u=2, r=2))
+                sbuf(("out0_rows", s), 4 * count * P, F32, "small", SMALL_BUFS)
+            rows = made["out0_rows", s][:].rearrange("p (r u j) -> p r u j", r=2, u=2)
+            nc.scalar.copy(out=rows[:, :, :, span(jt - first, P)],
+                           in_=made["out0", jt, s][:].rearrange("p (u r j) -> p r u j", u=2, r=2))
             if jt == first + count - 1:
                 for r in range(2):
-                    i0 = g * K + r * 2 * P
-                    dst = out_0[0, i0:i0 + 2 * P, first * P:(jt + 1) * P].rearrange("(p u) j -> p u j", u=2)
-                    nc.sync.dma_start(out=dst, in_=stage[:, r, :, :])
+                    dst = out_0[0, span(2 * s + r, 2 * P), first * P:(jt + 1) * P]
+                    nc.sync.dma_start(out=dst.rearrange("(p u) j -> p u j", u=2), in_=rows[:, r, :, :])
 
-        def dg_mm(b, h, a):
-            bank = sc_bank(("dg", b, h, a))
-            for g in range(2):
-                mx(bank[:], ("dya", b, g), E5M2, slice(a * P, (a + 1) * P), ("aq", b, h), E4M3, slice(g * K, (g + 1) * K), g == 0, g == 1)
-
-        def dg_ev(b, h, a):
+        def dg(b, h, a):
+            bank = scalar_bank("dg")
+            for s in range(2):
+                product(bank, ("dy_i", b, s), span(a, P), ("attn_mx", b, h), span(s, K), s == 0, s == 1)
             if a % 2 == 0:
-                T["dgs"] = sb.tile([P, 2 * K], F32, name="raw", tag="raw", bufs=RAW_BUFS, align_bytes=64)
-            nc.scalar.copy(out=T["dgs"][:, (a % 2) * K:(a % 2 + 1) * K], in_=T["dg", b, h, a][:])
+                sbuf("dg_rows", 2 * K, F32, "small", SMALL_BUFS)
+            nc.scalar.copy(out=made["dg_rows"][:, span(a % 2, K)], in_=bank[:])
             if a % 2 == 1:
-                dst = out_1[b, :, h * K:(h + 1) * K].rearrange("(m a) j -> m a j", a=4)
-                nc.sync.dma_start(out=dst[:, a - 1:a + 1, :], in_=T["dgs"][:].rearrange("p (a j) -> p a j", a=2))
+                dst = out_1[b, :, span(h, K)].rearrange("(m a) j -> m a j", a=4)
+                nc.sync.dma_start(out=dst[:, span(a // 2, 2), :], in_=made["dg_rows"][:].rearrange("p (a j) -> p a j", a=2))
 
         ident32 = sb.tile([P, P], F32, name="ident32")
         ident16 = sb.tile([P, P], BF16, name="ident16")
         lse_rows = sb.tile([P, P], F32, name="lse_rows")
-        neg_lse = sb.tile([P, 16], F32, name="neg_lse")
-        warm = sb.tile([P, 1], F32, name="warm")
-        nc.gpsimd.memset(lse_rows[:], 0.0)
-        nc.scalar.activation(out=warm[:], in_=lse_rows[:, 0:1], func=ACT.Exp)
+        neg_lse = sb.tile([P, STEPS], F32, name="neg_lse")
+        nc.vector.memset(lse_rows[:], 0.0)
         make_identity(nc, ident32[:])
         make_identity(nc, ident16[:])
 
-        def lse_load():
-            nc.sync.dma_start(out=lse_rows[0:16, :], in_=lse.rearrange("b (r p) -> (b r) p", p=P))
-
-        def lse_turn():
-            bank = sc_bank("lse")
-            nc.tensor.transpose(bank[:, 0:P], lse_rows[:], ident32[:])
-            nc.vector.tensor_scalar(out=neg_lse[:], in0=bank[:, 0:16], scalar1=-1.0, scalar2=None, op0=ALU.mult)
-
-        steps = [(b, jt) for b in range(B) for jt in range(4)] + [(b, jt) for jt in range(4, 8) for b in range(B)]
-        tiles = [(b, jt) for h in range(2) for b in range(B) for jt in range(4 * h, 4 * h + 4)]
-
-        def u_dy(b, g):
-            for a in range(4):
-                dy_mm(b, g, a); dy_ev(b, g, a)
-
-        def u_dya(b, g):
-            for pair in range(2):
-                dya_tr(b, g, pair); dya_ev(b, g, pair)
-
-        def u_aw(n):
-            aw_tr(*tiles[n]); aw_ev(*tiles[n])
-
-        def lgs(b, g, lo=0, hi=8):
-            for jt in range(lo, hi):
-                logits(b, jt, g); exp(b, jt, g)
-
-        load_w(0); load_go(0, 0, 0); load_w(1); load_go(0, 1, 0); load_go(0, 0, 1)
-        w_il(0, "V"); load_go(0, 1, 1); lse_load()
-        load_go_rows(1, 0); load_go_rows(1, 1); load_pos(0); load_qk(0, 0); load_dec()
-        go_il(0, 0, 0, "V"); w_il(1, "S")
-        w_q(0); go_q(0, 0, 0)
-        go_il(0, 1, 0, "V"); go_il(0, 0, 1, "S")
-        w_q(1); go_q(0, 1, 0)
-        go_il(0, 1, 1, "V")
-        u_dy(0, 0)
-        go_q(0, 0, 1); go_q(0, 1, 1)
+        load_w(0)
+        load_lse()
         lse_turn()
-        go_il(1, 0, 0, "V")
-        u_dy(0, 1)
-        go_il(1, 1, 0, "V"); go_q(1, 0, 0)
-        go_il(1, 0, 1, "V"); go_q(1, 1, 0)
-        load_g(0); load_pos(1); load_qk(0, 1)
-        u_dya(0, 0)
-        u_dya(0, 1)
-        go_il(1, 1, 1, E1)
+        load_go_group(0, 0)
+        load_w(1)
+        load_go_group(1, 0)
+        load_go_group(0, 1)
+        w_interleave(0, on_vector)
+        load_go_group(1, 1)
+        load_go_rows(0)
+        load_go_rows(1)
+        load_pos(0)
+        load_qk(0, 0, 0)
+        load_qk(0, 0, 1)
+        load_dec()
+        load_g(0)
+        load_pos(1)
+        load_qk(0, 1, 0)
+        load_qk(0, 1, 1)
+
+        go_interleave(0, 0, 0, on_vector)
+        w_interleave(1, on_scalar)
+        w_quantize(0)
+        go_quantize(0, 0, 0)
+        go_interleave(0, 1, 0, on_vector)
+        go_interleave(0, 0, 1, on_scalar)
+        w_quantize(1)
+        go_quantize(0, 1, 0)
+        go_interleave(0, 1, 1, on_vector)
+        dy_products(0, 0)
+        go_quantize(0, 0, 1)
+        go_quantize(0, 1, 1)
+        go_interleave(1, 0, 0, on_vector)
+        dy_products(0, 1)
+        go_interleave(1, 1, 0, on_vector)
+        go_quantize(1, 0, 0)
+        go_interleave(1, 0, 1, on_vector)
+        go_quantize(1, 1, 0)
+        dy_turn(0, 0)
+        dy_turn(0, 1)
+        go_interleave(1, 1, 1, on_scalar)
         load_g(1)
-        dyb_il(0, 0, "V"); go_q(1, 0, 1)
-        u_dy(1, 0)
-        dyb_il(0, 1, "V"); go_q(1, 1, 1); dyb_q(0, 0); dya_q(0, 0); dyb_q(0, 1); dya_q(0, 1)
-        u_dy(1, 1)
-        dyb_il(1, 0, "V")
-        u_dya(1, 0)
-        g_add(0); dyb_q(1, 0)
-        lgs(0, 0)
-        load_qk(1, 0)
-        u_dya(1, 1)
-        g_il(0, 0, "V"); dya_q(1, 0); g_il(0, 1, E2); g_q(0, 0)
-        lgs(0, 1)
-        load_qk(1, 1)
-        dyb_il(1, 1, "V"); g_q(0, 1); dya_q(1, 1); g_add(1); g_il(1, 0, "V"); g_il(1, 1, E3)
-        dattn(0, 0, 0); dattn(0, 0, 1); dattn(0, 1, 0)
-        g_q(1, 0); g_q(1, 1); dyb_q(1, 1)
-        late = [(1, jt, 0) for jt in range(PRE)]
-        late = late + [u for u in [(1, jt, g) for jt in range(8) for g in range(2)] if u not in late]
-        for k in range(PRE):
-            logits(*late[k]); exp(*late[k])
-        dg_units = [(b, h, a) for h in range(2) for b in range(B) for a in range(4)]
-        o0_units = [(jt, g) for jt in range(8) for g in range(2)]
-        done = {"late": PRE, "dg": 0, "turn": 0, "o0": 0}
-        for k in range(3):
-            cast(*tiles[k], CAST[k])
-        for n in range(17):
-            if n < 16:
-                col_sum(*steps[n], 0)
+        load_qk(1, 0, 0)
+        dy_c_interleave(0, 0)
+        go_quantize(1, 0, 1)
+        dy_products(1, 0)
+        dy_c_interleave(0, 1)
+        go_quantize(1, 1, 1)
+        dy_c_quantize(0, 0)
+        dy_i_quantize(0, 0)
+        dy_c_quantize(0, 1)
+        dy_i_quantize(0, 1)
+        dy_products(1, 1)
+        dy_c_interleave(1, 0)
+        dy_turn(1, 0)
+        g_add(0)
+        dy_c_quantize(1, 0)
+        probabilities_in_batches([(0, jt, 0) for jt in range(TILES)])
+        load_qk(1, 0, 1)
+        load_qk(1, 1, 0)
+        dy_turn(1, 1)
+        g_interleave(0, 0)
+        dy_i_quantize(1, 0)
+        g_interleave(0, 1)
+        g_quantize(0, 0)
+        probabilities_in_batches([(0, jt, 1) for jt in range(TILES)])
+        load_qk(1, 1, 1)
+        dy_c_interleave(1, 1)
+        g_quantize(0, 1)
+        g_add(1)
+        dy_i_quantize(1, 1)
+        g_interleave(1, 0)
+        g_interleave(1, 1)
+        g_quantize(1, 0)
+        g_quantize(1, 1)
+        dy_c_quantize(1, 1)
+
+        steps = [(b, jt) for b in range(B) for jt in range(4)] + [(b, jt) for jt in range(4, TILES) for b in range(B)]
+        logits_left = [(1, jt, 0) for jt in range(EARLY_LOGITS)]
+        logits_left = logits_left + [(1, jt, s) for jt in range(TILES) for s in range(2) if (1, jt, s) not in logits_left]
+        dattn(*steps[0], 0)
+        dattn(*steps[0], 1)
+        dattn(*steps[1], 0)
+        probabilities_in_batches(logits_left[:EARLY_LOGITS])
+        logits_left = logits_left[EARLY_LOGITS:]
+
+        turn_order = [(b, jt) for h in range(2) for b in range(B) for jt in range(4 * h, 4 * h + 4)]
+        turns_in_step = [0] + 2 * list(TURNS_OF_A_HALF) + [0] * STEPS
+        single_turn_steps = [n for n, count in enumerate(turns_in_step) if count == 1]
+        quantize_in_step = {n + 1: (k % B, k // B) for k, n in enumerate(single_turn_steps)}
+
+        def round_in_order(m):
+            attn_round(*turn_order[m], on_scalar if m % SCALAR_ROUNDS == SCALAR_ROUNDS - 1 else on_gpsimd)
+
+        for m in range(STAGING_BUFS):
+            round_in_order(m)
+        dg_ready, out0_ready = [], []
+        for n in range(STEPS + 1):
+            if n >= 2 and steps[n - 2][0] == B - 1:
+                out0_ready = out0_ready + [(steps[n - 2][1], s) for s in range(2)]
+            turned = sum(turns_in_step[:n])
+            turns = range(turned, turned + turns_in_step[n])
+            room = SIDE_UNITS + (n in quantize_in_step) - len(turns) // 2
+            logits_now, logits_left = logits_left[:LOGIT_BATCH], logits_left[LOGIT_BATCH:]
+            room = room - len(logits_now)
+            share = min(room, len(out0_ready), max(1, room - len(dg_ready)))
+            out0_now, out0_ready = out0_ready[:share], out0_ready[share:]
+            dg_now, dg_ready = dg_ready[:room - share], dg_ready[room - share:]
+
+            if n < STEPS:
+                partial_sum(*steps[n], 0)
             if n > 0:
-                dsoft(*steps[n - 1], 0)
-            if n in AQ:
-                attn_q(*AQ[n])
-            if 0 < n < 16:
+                ds(*steps[n - 1], 0)
+            if 0 < n < STEPS:
                 dattn(*steps[n], 1)
-            for k in range(DGS.get(n, 0)):
-                bb, hh, aa = dg_units[done["dg"]]
-                done["dg"] = done["dg"] + 1
-                dg_mm(bb, hh, aa); dg_ev(bb, hh, aa)
-            if 1 < n + 1 < 16:
+            if n in quantize_in_step:
+                attn_quantize(*quantize_in_step[n])
+                dg_ready = dg_ready + [(*quantize_in_step[n], a) for a in range(4)]
+            for unit in dg_now:
+                dg(*unit)
+            if 0 < n < STEPS - 1:
                 dattn(*steps[n + 1], 0)
-            if n < 16:
-                col_sum(*steps[n], 1)
+            if n < STEPS:
+                partial_sum(*steps[n], 1)
             if n > 0:
-                dsoft(*steps[n - 1], 1)
-            if n < 16:
-                col_total(*steps[n])
-            for k in range(TURN.get(n, 0)):
-                u_aw(done["turn"])
-                done["turn"] = done["turn"] + 1
-            for k in range(LATE.get(n, 0)):
-                u = late[done["late"]]
-                done["late"] = done["late"] + 1
-                logits(*u); exp(*u)
-            for m in range(done["turn"] - TURN.get(n, 0), done["turn"]):
-                if m + 3 < 16:
-                    cast(*tiles[m + 3], CAST[m + 3])
-            for k in range(O0S.get(n, 0)):
-                jt, g = o0_units[done["o0"]]
-                done["o0"] = done["o0"] + 1
-                o0_tr(jt, g); o0_ev(jt, g)
-            if n == 15:
-                o0_tr(7, 0, [0]); o0_tr(7, 1, [0])
-        for g in range(2):
-            o0_tr(7, g, [1]); o0_ev(7, g)
+                ds(*steps[n - 1], 1)
+            if n < STEPS:
+                total_sum(*steps[n])
+            for m in turns:
+                attn_turn(*turn_order[m])
+            probabilities(logits_now)
+            for m in turns:
+                if m + STAGING_BUFS < STEPS:
+                    round_in_order(m + STAGING_BUFS)
+            for jt, s in out0_now:
+                for b in range(B - 1 if jt in GPSIMD_SUMS else 0, B):
+                    out0_turn(jt, s, b)
+                out0_store(jt, s)
+            if n == STEPS - 1:
+                for s in range(2):
+                    out0_turn(TILES - 1, s, 0)
+        for s in range(2):
+            out0_turn(TILES - 1, s, 1)
+            out0_store(TILES - 1, s)

@@ -108,7 +108,7 @@ def tile_nonlocalblock_pa_v_kernel(
 
         def interleave(copy, key, src):
             tile = sbuf(key, 4 * K, BF16, "staging", STAGING_BUFS)
-            copy(tile[:].rearrange("p (n k t) -> p n t k", k=4, t=4), src.rearrange("p t (n k) -> p n t k", k=4))
+            copy(tile[:].rearrange("p (n k t) -> p n t k", k=8, t=4), src.rearrange("p t (n k) -> p n t k", k=8))
 
         def operand(key, fmt, width, tag, bufs):
             codes = sb.tile([P, width], U32, name=tag + "_codes", tag=tag + "_codes", bufs=bufs, align_bytes=64)

from contextlib import ExitStack

import concourse.mybir as mybir
from concourse.masks import make_identity

B, C, IC, N = 2, 1024, 512, 1024
FLOPS = 3 * 2 * B * N * N * IC
BYTES = 2 * (B * IC * N + N * N + IC * N + C * IC + B * C * N) + 4 * (B * N * N + B * N + N * N + B * IC * N)

F32 = mybir.dt.float32
BF16 = mybir.dt.bfloat16
U32 = mybir.dt.uint32
U8 = mybir.dt.uint8
E4M3 = mybir.dt.float8_e4m3fn_x4
E5M2 = mybir.dt.float8_e5m2_x4
ALU = mybir.AluOpType
ACT = mybir.ActivationFunctionType

P = 128
K = 512
TILES = N // P
STEPS = B * TILES

SMALL_BUFS = 5
WIDE_BUFS = 4
QK_BUFS = 5
STAGING_BUFS = 3
MOVING_BUFS = 3
DATTN_BANKS = 4
SCALAR_BANKS = 8 - DATTN_BANKS

LOGIT_BATCH = 2
EARLY_LOGITS = 6
SIDE_UNITS = 3
SCALAR_ROUNDS = 3
TURNS_OF_A_HALF = (2, 2, 1, 2, 1)
GPSIMD_SUMS = range(TILES // 2, TILES - 1)
OUT0_RUNS = [(jt - jt % 2, 2) for jt in range(TILES - 2)] + [(TILES - 2, 1), (TILES - 1, 1)]


def tile_nonlocalblock_pa_v_kernel(
    tc, theta, phi, g_proj, pos_embedding, pos_embedding_decoder, w_mask, x, qk, lse, grad_out, out_0, out_1
):
    nc = tc.nc
    go_hbm = grad_out.rearrange("b o h w -> b o (h w)")
    dec_hbm = pos_embedding_decoder.rearrange("b c h w -> b c (h w)")

    with ExitStack() as ctx:
        sb = ctx.enter_context(tc.tile_pool(name="sb", bufs=1))
        ps = ctx.enter_context(tc.psum_pool(name="ps", bufs=1))
        ctx.enter_context(tc.manual_schedule())

        made = {}

        def span(k, width):
            return slice(k * width, (k + 1) * width)

        def four_rows(ap):
            return ap.rearrange("p (t n) -> p t n", t=4)

        def sbuf(key, width, dtype, tag, bufs):
            made[key] = sb.tile([P, width], dtype, name=tag, tag=tag, bufs=bufs, align_bytes=64)
            return made[key]

        def scalar_bank(key):
            made[key] = ps.tile([P, K], F32, name="scalar_bank", tag="scalar_bank", bufs=SCALAR_BANKS)
            return made[key]

        def load(key, src, dtype, tag, bufs):
            rows, width = src.shape[0] // P, src.shape[1]
            tile = sbuf(key, rows * width, dtype, tag, bufs)
            nc.sync.dma_start(out=tile[:].rearrange("p (t n) -> p t n", t=rows),
                              in_=src.rearrange("(p t) n -> p t n", t=rows))

        def load_w(q):
            load(("w", q), w_mask[span(q, K), :], BF16, "small", SMALL_BUFS)

        def load_go_group(q, s):
            load(("go", 0, q, s), go_hbm[0, span(q, K), span(s, K)], BF16, "small", SMALL_BUFS)

        def load_go_rows(q):
            load(("go", 1, q), go_hbm[1, span(q, K), :], BF16, "wide", WIDE_BUFS)

        def load_dec():
            load("dec", dec_hbm[0], BF16, "wide", WIDE_BUFS)

        def load_g(b):
            load(("g", b), g_proj[b], BF16, "wide", WIDE_BUFS)

        def load_pos(s):
            for r in range(2):
                load(("pos", s, r), pos_embedding[0, span(2 * s + r, 2 * P), :], BF16, "pos", 4)

        def load_qk(b, s, r):
            load(("qk", b, s, r), qk[b, span(2 * s + r, 2 * P), :], F32, "qk", QK_BUFS)

        def load_lse():
            nc.sync.dma_start(out=lse_rows[0:STEPS, :], in_=lse.rearrange("b (jt p) -> (b jt) p", p=P))

        def on_vector(out, in_):
            nc.vector.tensor_copy(out=out, in_=in_)

        def on_scalar(out, in_):
            nc.scalar.copy(out=out, in_=in_)

        def on_gpsimd(out, in_):
            nc.gpsimd.tensor_scalar(out=out, in0=in_, scalar1=1.0, scalar2=0.0, op0=ALU.mult, op1=ALU.add)

        def interleave(copy, key, src):
            tile = sbuf(key, 4 * K, BF16, "staging", STAGING_BUFS)
            copy(tile[:].rearrange("p (n k t) -> p n t k", k=8, t=4), src.rearrange("p t (n k) -> p n t k", k=8))

        def operand(key, fmt, width, tag, bufs):
            codes = sb.tile([P, width], U32, name=tag + "_codes", tag=tag + "_codes", bufs=bufs, align_bytes=64)
            scales = sb.tile([P, width], U8, name=tag + "_scales", tag=tag + "_scales", bufs=bufs, align_bytes=64)
            made[key] = (codes, scales, fmt)

        def quantize(key, cols, src):
            codes, scales, fmt = made[key]
            nc.vector.quantize_mx(out=codes[:, cols].bitcast(fmt), scales=scales[:, cols], in_=src[:])

        def product(out, lhs_key, lhs_cols, rhs_key, rhs_cols, start, stop):
            lhs_codes, lhs_scales, lhs_fmt = made[lhs_key]
            rhs_codes, rhs_scales, rhs_fmt = made[rhs_key]
            nc.tensor.matmul_mx(out=out[:], lhsT=lhs_codes[:, lhs_cols].bitcast(lhs_fmt), lhsT_scale=lhs_scales[:, lhs_cols],
                                rhs=rhs_codes[:, rhs_cols].bitcast(rhs_fmt), rhs_scale=rhs_scales[:, rhs_cols],
                                start=start, stop=stop)

        def w_interleave(q, copy):
            tile = sbuf(("w_in", q), 4 * K, BF16, "staging", STAGING_BUFS)
            copy(tile[:].rearrange("p (a m t) -> p a m t", a=4, t=4),
                 made["w", q][:].rearrange("p (t m a) -> p a m t", t=4, a=4))

        def w_quantize(q):
            operand(("w_mx", q), E4M3, K, "w", 2)
            quantize(("w_mx", q), span(0, K), made["w_in", q])

        def go_interleave(b, q, s, copy):
            src = four_rows(made["go", 0, q, s][:]) if b == 0 else four_rows(made["go", 1, q][:])[:, :, span(s, K)]
            interleave(copy, ("go_in", b, q, s), src)

        def go_quantize(b, q, s):
            if q == 0:
                operand(("go_mx", b, s), E5M2, 2 * K, "moving", MOVING_BUFS)
            quantize(("go_mx", b, s), span(q, K), made["go_in", b, q, s])

        def g_add(b):
            nc.vector.tensor_tensor(out=made["g", b][:], in0=made["g", b][:], in1=made["dec"][:], op=ALU.add)

        def g_interleave(b, h):
            interleave(on_vector, ("g_in", b, h), four_rows(made["g", b][:])[:, :, span(h, K)])

        def g_quantize(b, h):
            operand(("g_mx", b, h), E4M3, K, "g", 4)
            quantize(("g_mx", b, h), span(0, K), made["g_in", b, h])

        def dy_products(b, s):
            for a in range(4):
                bank = scalar_bank("dy")
                for q in range(2):
                    product(bank, ("w_mx", q), span(a, P), ("go_mx", b, s), span(q, K), q == 0, q == 1)
                if a == 0:
                    sbuf(("dy_bf", b, s), 4 * K, BF16, "small", SMALL_BUFS)
                nc.scalar.copy(out=made["dy_bf", b, s][:, span(a, K)].rearrange("p (u v) -> p u v", u=2),
                               in_=bank[:].rearrange("p (v u) -> p u v", u=2))

        def dy_c_interleave(b, s):
            interleave(on_vector, ("dy_c_in", b, s), four_rows(made["dy_bf", b, s][:]))

        def dy_c_quantize(b, s):
            operand(("dy_c", b, s), E5M2, K, "dy_c", 4)
            quantize(("dy_c", b, s), span(0, K), made["dy_c_in", b, s])

        def dy_turn(b, s):
            words = made["dy_bf", b, s][:].bitcast(F32)
            for pair in range(2):
                bank = scalar_bank("dy_words")
                for k in range(4):
                    nc.tensor.transpose(bank[:, span(k, P)], words[:, span(4 * pair + k, P)], ident32[:])
                if pair == 0:
                    sbuf(("dy_i_in", b, s), 4 * K, BF16, "small", SMALL_BUFS)
                dst = made["dy_i_in", b, s][:].bitcast(F32)[:, span(pair, K)]
                nc.scalar.copy(out=dst.rearrange("p (a m u) -> p a m u", a=2, u=2),
                               in_=bank[:].rearrange("p (a u m) -> p a m u", a=2, u=2))

        def dy_i_quantize(b, s):
            operand(("dy_i", b, s), E5M2, K, "dy_i", 4)
            quantize(("dy_i", b, s), span(0, K), made["dy_i_in", b, s])

        def lse_turn():
            bank = scalar_bank("lse")
            nc.tensor.transpose(bank[:, 0:P], lse_rows[:], ident32[:])
            nc.scalar.activation(out=neg_lse[:], in_=bank[:, 0:STEPS], func=ACT.Identity, scale=-1.0)

        def logit_blocks(kind, jt):
            return [made[kind + (k % 2,)][:, span(TILES * (k // 2) + jt, P)] for k in range(4)]

        def probabilities(units):
            for b, jt, s in units:
                bank = scalar_bank(("logits", b, jt, s))
                for k, block in enumerate(logit_blocks(("pos", s), jt)):
                    nc.tensor.matmul(bank[:, span(k, P)], lhsT=block, rhs=ident16[:], start=(k == 0), stop=False)
            for b, jt, s in units:
                bank = made["logits", b, jt, s]
                for k, block in enumerate(logit_blocks(("qk", b, s), jt)):
                    nc.tensor.matmul(bank[:, span(k, P)], lhsT=block, rhs=ident32[:], start=False, stop=(k == 3),
                                     is_transpose=True)
                if s == 0:
                    sbuf(("attn", b, jt), N, F32, "attn", STEPS)
                nc.scalar.activation(out=made["attn", b, jt][:, span(s, K)], in_=bank[:], func=ACT.Exp,
                                     bias=neg_lse[:, span(TILES * b + jt, 1)])

        def probabilities_in_batches(units):
            for k in range(0, len(units), LOGIT_BATCH):
                probabilities(units[k:k + LOGIT_BATCH])

        def attn_round(b, jt, copy):
            copy(sbuf(("attn_bf", b, jt), N, BF16, "staging", STAGING_BUFS)[:], made["attn", b, jt][:])

        def attn_turn(b, jt):
            bank = scalar_bank("attn_words")
            words = made["attn_bf", b, jt][:].bitcast(F32)
            for k in range(4):
                nc.tensor.transpose(bank[:, span(k, P)], words[:, span(k, P)], ident32[:])
            if jt % 4 == 0:
                sbuf(("attn_in", b, jt // 4), 8 * K, BF16, "wide", WIDE_BUFS)
            dst = made["attn_in", b, jt // 4][:].bitcast(F32).rearrange("p (s j u) -> p s j u", s=2, u=2)
            nc.scalar.copy(out=dst[:, :, span(jt % 4, P), :], in_=bank[:].rearrange("p (s u j) -> p s j u", s=2, u=2))

        def attn_quantize(b, h):
            operand(("attn_mx", b, h), E4M3, 2 * K, "moving", MOVING_BUFS)
            quantize(("attn_mx", b, h), span(0, 2 * K), made["attn_in", b, h])

        def dattn(b, jt, s):
            made["dattn", b, jt, s] = ps.tile([P, K], F32, name="dattn", tag="dattn", bufs=DATTN_BANKS)
            product(made["dattn", b, jt, s], ("g_mx", b, jt // 4), span(jt % 4, P), ("dy_c", b, s), span(0, K), True, True)

        def partial_sum(b, jt, s):
            if s == 0:
                made["partial", b, jt] = sb.tile([P, 2], F32, name="partial", tag="partial", bufs=4)
            products = sb.tile([P, K], F32, name="products", tag="products", bufs=1)
            nc.vector.scalar_tensor_tensor(out=products[:], in0=made["dattn", b, jt, s][:], scalar=1.0,
                                           in1=made["attn", b, jt][:, span(s, K)], op0=ALU.mult, op1=ALU.mult,
                                           accum_out=made["partial", b, jt][:, span(s, 1)])

        def total_sum(b, jt):
            made["total", b, jt] = sb.tile([P, 1], F32, name="total", tag="total", bufs=4)
            nc.vector.tensor_reduce(out=made["total", b, jt][:], in_=made["partial", b, jt][:],
                                    axis=mybir.AxisListType.X, op=ALU.add)

        def ds(b, jt, s):
            half = made["attn", b, jt][:, span(s, K)]
            nc.vector.scalar_tensor_tensor(out=half, in0=made["dattn", b, jt, s][:], scalar=made["total", b, jt][:],
                                           in1=half, op0=ALU.subtract, op1=ALU.mult)
            if b == B - 1 and jt in GPSIMD_SUMS:
                nc.gpsimd.tensor_tensor(out=half, in0=half, in1=made["attn", 0, jt][:, span(s, K)], op=ALU.add)

        def out0_turn(jt, s, b):
            opens = b == 0 or jt in GPSIMD_SUMS
            bank = scalar_bank(("out0", jt, s)) if opens else made["out0", jt, s]
            for k in range(4):
                nc.tensor.matmul(bank[:, span(k, P)], lhsT=made["attn", b, jt][:, span(4 * s + k, P)], rhs=ident32[:],
                                 start=(opens and k == 0), stop=(b == B - 1 and k == 3), is_transpose=True)

        def out0_store(jt, s):
            first, count = OUT0_RUNS[jt]
            if jt == first:
                sbuf(("out0_rows", s), 4 * count * P, F32, "small", SMALL_BUFS)
            rows = made["out0_rows", s][:].rearrange("p (r u j) -> p r u j", r=2, u=2)
            nc.scalar.copy(out=rows[:, :, :, span(jt - first, P)],
                           in_=made["out0", jt, s][:].rearrange("p (u r j) -> p r u j", u=2, r=2))
            if jt == first + count - 1:
                for r in range(2):
                    dst = out_0[0, span(2 * s + r, 2 * P), first * P:(jt + 1) * P]
                    nc.sync.dma_start(out=dst.rearrange("(p u) j -> p u j", u=2), in_=rows[:, r, :, :])

        def dg(b, h, a):
            bank = scalar_bank("dg")
            for s in range(2):
                product(bank, ("dy_i", b, s), span(a, P), ("attn_mx", b, h), span(s, K), s == 0, s == 1)
            if a % 2 == 0:
                sbuf("dg_rows", 2 * K, F32, "small", SMALL_BUFS)
            nc.scalar.copy(out=made["dg_rows"][:, span(a % 2, K)], in_=bank[:])
            if a % 2 == 1:
                dst = out_1[b, :, span(h, K)].rearrange("(m a) j -> m a j", a=4)
                nc.sync.dma_start(out=dst[:, span(a // 2, 2), :], in_=made["dg_rows"][:].rearrange("p (a j) -> p a j", a=2))

        ident32 = sb.tile([P, P], F32, name="ident32")
        ident16 = sb.tile([P, P], BF16, name="ident16")
        lse_rows = sb.tile([P, P], F32, name="lse_rows")
        neg_lse = sb.tile([P, STEPS], F32, name="neg_lse")
        nc.vector.memset(lse_rows[:], 0.0)
        make_identity(nc, ident32[:])
        make_identity(nc, ident16[:])

        load_w(0)
        load_lse()
        lse_turn()
        load_go_group(0, 0)
        load_w(1)
        load_go_group(1, 0)
        load_go_group(0, 1)
        w_interleave(0, on_vector)
        load_go_group(1, 1)
        load_go_rows(0)
        load_go_rows(1)
        load_pos(0)
        load_qk(0, 0, 0)
        load_qk(0, 0, 1)
        load_dec()
        load_g(0)
        load_pos(1)
        load_qk(0, 1, 0)
        load_qk(0, 1, 1)

        go_interleave(0, 0, 0, on_vector)
        w_interleave(1, on_scalar)
        w_quantize(0)
        go_quantize(0, 0, 0)
        go_interleave(0, 1, 0, on_vector)
        go_interleave(0, 0, 1, on_scalar)
        w_quantize(1)
        go_quantize(0, 1, 0)
        go_interleave(0, 1, 1, on_vector)
        dy_products(0, 0)
        go_quantize(0, 0, 1)
        go_quantize(0, 1, 1)
        go_interleave(1, 0, 0, on_vector)
        dy_products(0, 1)
        go_interleave(1, 1, 0, on_vector)
        go_quantize(1, 0, 0)
        go_interleave(1, 0, 1, on_vector)
        go_quantize(1, 1, 0)
        dy_turn(0, 0)
        dy_turn(0, 1)
        go_interleave(1, 1, 1, on_scalar)
        load_g(1)
        load_qk(1, 0, 0)
        dy_c_interleave(0, 0)
        go_quantize(1, 0, 1)
        dy_products(1, 0)
        dy_c_interleave(0, 1)
        go_quantize(1, 1, 1)
        dy_c_quantize(0, 0)
        dy_i_quantize(0, 0)
        dy_c_quantize(0, 1)
        dy_i_quantize(0, 1)
        dy_products(1, 1)
        dy_c_interleave(1, 0)
        dy_turn(1, 0)
        g_add(0)
        dy_c_quantize(1, 0)
        probabilities_in_batches([(0, jt, 0) for jt in range(TILES)])
        load_qk(1, 0, 1)
        load_qk(1, 1, 0)
        dy_turn(1, 1)
        g_interleave(0, 0)
        dy_i_quantize(1, 0)
        g_interleave(0, 1)
        g_quantize(0, 0)
        probabilities_in_batches([(0, jt, 1) for jt in range(TILES)])
        load_qk(1, 1, 1)
        dy_c_interleave(1, 1)
        g_quantize(0, 1)
        g_add(1)
        dy_i_quantize(1, 1)
        g_interleave(1, 0)
        g_interleave(1, 1)
        g_quantize(1, 0)
        g_quantize(1, 1)
        dy_c_quantize(1, 1)

        steps = [(b, jt) for b in range(B) for jt in range(4)] + [(b, jt) for jt in range(4, TILES) for b in range(B)]
        logits_left = [(1, jt, 0) for jt in range(EARLY_LOGITS)]
        logits_left = logits_left + [(1, jt, s) for jt in range(TILES) for s in range(2) if (1, jt, s) not in logits_left]
        dattn(*steps[0], 0)
        dattn(*steps[0], 1)
        dattn(*steps[1], 0)
        probabilities_in_batches(logits_left[:EARLY_LOGITS])
        logits_left = logits_left[EARLY_LOGITS:]

        turn_order = [(b, jt) for h in range(2) for b in range(B) for jt in range(4 * h, 4 * h + 4)]
        turns_in_step = [0] + 2 * list(TURNS_OF_A_HALF) + [0] * STEPS
        single_turn_steps = [n for n, count in enumerate(turns_in_step) if count == 1]
        quantize_in_step = {n + 1: (k % B, k // B) for k, n in enumerate(single_turn_steps)}

        def round_in_order(m):
            attn_round(*turn_order[m], on_scalar if m % SCALAR_ROUNDS == SCALAR_ROUNDS - 1 else on_gpsimd)

        for m in range(STAGING_BUFS):
            round_in_order(m)
        dg_ready, out0_ready = [], []
        for n in range(STEPS + 1):
            if n >= 2 and steps[n - 2][0] == B - 1:
                out0_ready = out0_ready + [(steps[n - 2][1], s) for s in range(2)]
            turned = sum(turns_in_step[:n])
            turns = range(turned, turned + turns_in_step[n])
            room = SIDE_UNITS + (n in quantize_in_step) - len(turns) // 2
            logits_now, logits_left = logits_left[:LOGIT_BATCH], logits_left[LOGIT_BATCH:]
            room = room - len(logits_now)
            share = min(room, len(out0_ready), max(1, room - len(dg_ready)))
            out0_now, out0_ready = out0_ready[:share], out0_ready[share:]
            dg_now, dg_ready = dg_ready[:room - share], dg_ready[room - share:]

            if n < STEPS:
                partial_sum(*steps[n], 0)
            if n > 0:
                ds(*steps[n - 1], 0)
            if 0 < n < STEPS:
                dattn(*steps[n], 1)
            if n in quantize_in_step:
                attn_quantize(*quantize_in_step[n])
                dg_ready = dg_ready + [(*quantize_in_step[n], a) for a in range(4)]
            for unit in dg_now:
                dg(*unit)
            if 0 < n < STEPS - 1:
                dattn(*steps[n + 1], 0)
            if n < STEPS:
                partial_sum(*steps[n], 1)
            if n > 0:
                ds(*steps[n - 1], 1)
            if n < STEPS:
                total_sum(*steps[n])
            for m in turns:
                attn_turn(*turn_order[m])
            probabilities(logits_now)
            for m in turns:
                if m + STAGING_BUFS < STEPS:
                    round_in_order(m + STAGING_BUFS)
            for jt, s in out0_now:
                for b in range(B - 1 if jt in GPSIMD_SUMS else 0, B):
                    out0_turn(jt, s, b)
                out0_store(jt, s)
            if n == STEPS - 1:
                for s in range(2):
                    out0_turn(TILES - 1, s, 0)
        for s in range(2):
            out0_turn(TILES - 1, s, 1)
            out0_store(TILES - 1, s)
